import numpy as np
import ml_dtypes


def mxq(x, axis, fmt="e4m3"):
    dtype, down = {"e4m3": (ml_dtypes.float8_e4m3fn, 7), "e5m2": (ml_dtypes.float8_e5m2, 14)}[fmt]
    v = np.moveaxis(np.asarray(x, np.float32).astype(ml_dtypes.bfloat16).astype(np.float64), axis, -1)
    blocks = v.reshape(v.shape[:-1] + (-1, 32))
    amax = np.abs(blocks).max(-1, keepdims=True)
    byte = np.maximum(np.where(amax > 0, np.frexp(amax)[1] - 1 + 127, 0) - down, 1)
    scale = np.exp2(byte - 127.0)
    codes = (blocks / scale).astype(np.float32).astype(dtype).astype(np.float64)
    return np.moveaxis((codes * scale).reshape(v.shape), -1, axis)


WIDE = False


def mx_kscale(k):
    if not WIDE:
        return np.ones(k)
    levels = np.array([10, -10, 5, -5, 0])
    if k % 512:
        return np.exp2(np.random.permutation(np.resize(levels, k // 32))).repeat(32)
    a = np.empty((k // 512, 16))
    for p in range(k // 512):
        a[p, :8] = np.random.permutation(np.resize(levels, 8))
        for g in range(8):
            far = levels[np.abs(levels - a[p, g]) >= 10]
            a[p, g + 8] = far[np.random.randint(len(far))]
    return np.exp2(a.ravel()).repeat(32)


BF16 = ml_dtypes.bfloat16


def bf(x):
    return np.asarray(x, np.float32).astype(BF16)


def f64(x):
    return np.asarray(x).astype(np.float64)


B, CL, CH, CK, CV, CO, H, W = 2, 1024, 2048, 256, 512, 1024, 24, 24
N = H * W
PSP = (1, 3, 6, 8)
EPS = 1e-5


def psp(x):
    b, c, h, w = x.shape
    return np.concatenate(
        [x.reshape(b, c, s, h // s, s, w // s).mean(axis=(3, 5)).reshape(b, c, s * s) for s in PSP], axis=2)


def setup_inputs():
    s = mx_kscale(CL)
    return {"low_feats": bf(np.random.standard_normal((B, CL, H, W)) * s[None, :, None, None]),
            "wk": bf(np.random.standard_normal((CK, CL)) * 2.5 / np.sqrt(CL) / s[None, :]),
            "bk": bf(np.random.standard_normal(CK) * 0.3),
            "gk": bf(np.random.uniform(0.5, 1.5, CK)),
            "bek": bf(np.random.standard_normal(CK) * 0.3),
            "mk": bf(np.random.standard_normal(CK) * 0.3),
            "vk": bf(np.random.uniform(0.5, 1.5, CK)),
            "wv": bf(np.random.standard_normal((CV, CL)) * 3.0 / np.sqrt(CL) / s[None, :]),
            "bv": bf(np.random.standard_normal(CV) * 0.3)}


def reference(low_feats, wk, bk, gk, bek, mk, vk, wv, bv):
    xq = mxq(f64(low_feats).reshape(B, CL, N), 1, "e4m3")
    v = (mxq(f64(wv), 1, "e4m3") @ xq) + f64(bv)[None, :, None]
    value = psp(v.reshape(B, CV, H, W)).transpose(0, 2, 1)
    u = (mxq(f64(wk), 1, "e4m3") @ xq) + f64(bk)[None, :, None]
    sc = f64(gk) / np.sqrt(f64(vk) + EPS)
    r = np.maximum((u - f64(mk)[None, :, None]) * sc[None, :, None] + f64(bek)[None, :, None], 0.0)
    key = psp(r.reshape(B, CK, H, W))
    return value, key

@@ -1,0 +1,460 @@
+from contextlib import ExitStack
+
+import concourse.mybir as mybir
+from concourse.masks import make_identity
+
+F32 = mybir.dt.float32
+BF16 = mybir.dt.bfloat16
+U32 = mybir.dt.uint32
+U8 = mybir.dt.uint8
+FP8X4 = mybir.dt.float8_e4m3fn_x4
+ALU = mybir.AluOpType
+ACT = mybir.ActivationFunctionType
+AX = mybir.AxisListType
+
+P = 128
+NB = 2
+NPX = 576
+NX = NB * NPX
+CH = 768
+NLOC = 110
+EPS = 1e-5
+FLOPS = 2 * 768 * 1024 * 1152
+PX_STARTS = (0, 128, 256, 384, 448)
+
+
+def tile_afnb_pa_kernel(tc, low_feats, wk, bk, gk, bek, mk, vk, wv, bv, out_0, out_1):
+    nc = tc.nc
+    with ExitStack() as ctx:
+        keep = ctx.enter_context(tc.tile_pool(name="keep", bufs=1))
+        work = ctx.enter_context(tc.tile_pool(name="work", bufs=2))
+        vpool = ctx.enter_context(tc.tile_pool(name="vpool", bufs=3))
+        psum = ctx.enter_context(tc.psum_pool(name="psum", bufs=1))
+        ctx.enter_context(tc.manual_schedule())
+
+        prm = keep.tile([P, P], BF16)
+        bvrow = keep.tile([P, 512], BF16)
+        w_sb = keep.tile([P, 6 * 1024], BF16)
+        xr = []
+        for b in range(NB):
+            row = []
+            for g in range(2):
+                xr_bg = keep.tile([P, 4, NPX], BF16, name="xr%d%d" % (b, g))
+                row.append(xr_bg)
+            xr.append(row)
+        ident_b = keep.tile([P, P], BF16)
+        ident_f = keep.tile([P, P], F32)
+        warm = keep.tile([P, 1], F32)
+        q8 = keep.tile([P, 8, 24], BF16)
+        q6 = keep.tile([P, 6, 24], BF16)
+        q3 = keep.tile([P, 3, 24], BF16)
+        member = keep.tile([P, 24, 24], BF16)
+        mflat = member[:].rearrange("p h w -> p (h w)")
+        mtail = keep.tile([P, P], BF16)
+        pmat = keep.tile([P, 5, P], F32)
+        ones = keep.tile([P, P], BF16)
+        wloc = keep.tile([P, NLOC], F32)
+        rtmp = keep.tile([P, NLOC], F32)
+        rs = keep.tile([P, 1], F32)
+        sums = keep.tile([P, NB, 4, P], F32)
+        prmt = keep.tile([P, 10], F32)
+        sc = keep.tile([P, 2], F32)
+        bi = keep.tile([P, 2], F32)
+        bvb = keep.tile([P, 512], F32)
+        wf = w_sb[:].bitcast(F32)
+        wg = keep.tile([P, 2 * CH * 4], BF16, align_bytes=64)
+        wgf = wg[:].bitcast(F32).rearrange("p (g c u) -> p g c u", g=2, u=2)
+        wc = keep.tile([P, 2 * CH], U32, align_bytes=64)
+        wsc = keep.tile([P, 2 * CH], U8, align_bytes=64)
+        xg = keep.tile([P, 2 * NX * 4], BF16, align_bytes=64)
+        xc = keep.tile([P, 2 * NX], U32, align_bytes=64)
+        xs = keep.tile([P, 2 * NX], U8, align_bytes=64)
+
+        def load_x(b, g):
+            nc.sync.dma_start(
+                out=xr[b][g][:],
+                in_=low_feats[b, 512 * g : 512 * g + 512].rearrange("(q t) h w -> q t (h w)", t=4),
+            )
+
+        def load_w(r0, n_blocks, rows):
+            nc.sync.dma_start(
+                out=w_sb[:, 1024 * r0 : 1024 * (r0 + n_blocks)].rearrange(
+                    "p (r k) -> p r k", k=1024
+                ),
+                in_=rows.rearrange("(r p) k -> p r k", p=P),
+            )
+
+        def weight_transposes(r, bank):
+            pw = psum.tile([P, 2, 2, P], F32, tag=bank, name="pw%d" % r)
+            for g in range(2):
+                for u in range(2):
+                    c0 = 512 * r + 256 * g
+                    nc.tensor.transpose(
+                        out=pw[:, g, u, :], in_=wf[:, c0 + u : c0 + 256 : 2], identity=ident_f[:]
+                    )
+            return pw
+
+        def weight_copy(r, pw, on_vector):
+            dst = wgf[:, :, P * r : P * r + P, :]
+            src = pw[:].rearrange("p g u c -> p g c u")
+            if on_vector:
+                nc.vector.tensor_copy(out=dst, in_=src)
+            else:
+                nc.scalar.copy(out=dst, in_=src)
+
+        def weight_quant(c0, c1):
+            for g in range(2):
+                lo = g * CH + c0
+                hi = g * CH + c1
+                nc.vector.quantize_mx(
+                    out=wc[:, lo:hi].bitcast(FP8X4),
+                    scales=wsc[:, lo:hi],
+                    in_=wg[:, 4 * lo : 4 * hi],
+                )
+
+        def regroup(b, g, a0, a1, on_vector):
+            base = g * NX + NPX * b
+            dst = xg[:, 4 * (base + a0) : 4 * (base + a1)].rearrange(
+                "p (c i t) -> p c t i", i=4, t=4
+            )
+            src = xr[b][g][:, :, a0:a1].rearrange("p t (c i) -> p c t i", i=4)
+            if on_vector == "gpsimd":
+                nc.gpsimd.tensor_scalar(
+                    out=dst, in0=src, scalar1=1.0, scalar2=0.0, op0=ALU.mult, op1=ALU.add
+                )
+            elif on_vector:
+                nc.vector.tensor_copy(out=dst, in_=src)
+            else:
+                nc.scalar.copy(out=dst, in_=src)
+
+        def quant_x(g, lo, hi):
+            lo = g * NX + lo
+            hi = g * NX + hi
+            nc.vector.quantize_mx(
+                out=xc[:, lo:hi].bitcast(FP8X4),
+                scales=xs[:, lo:hi],
+                in_=xg[:, 4 * lo : 4 * hi],
+            )
+
+        def mx_group(out, blk, lo, n):
+            for g in range(2):
+                w0 = g * CH + P * blk
+                x0 = g * NX + lo
+                nc.tensor.matmul_mx(
+                    out=out,
+                    lhsT=wc[:, w0 : w0 + P].bitcast(FP8X4),
+                    lhsT_scale=wsc[:, w0 : w0 + P],
+                    rhs=xc[:, x0 : x0 + n].bitcast(FP8X4),
+                    rhs_scale=xs[:, x0 : x0 + n],
+                    start=(g == 0),
+                    stop=(g == 1),
+                )
+
+        def px_group(out, lo):
+            for g in range(2):
+                x0 = g * NX + lo
+                nc.tensor.matmul_mx(
+                    out=out,
+                    lhsT=xc[:, x0 : x0 + P].bitcast(FP8X4),
+                    lhsT_scale=xs[:, x0 : x0 + P],
+                    rhs=wc[:, g * CH : g * CH + 256].bitcast(FP8X4),
+                    rhs_scale=wsc[:, g * CH : g * CH + 256],
+                    start=(g == 0),
+                    stop=(g == 1),
+                )
+
+        def pool_pair(src8, dst8, src6, dst6):
+            nc.vector.tensor_reduce(out=dst8, in_=src8, axis=AX.XY, op=ALU.add)
+            nc.vector.tensor_reduce(out=dst6, in_=src6, axis=AX.XY, op=ALU.add)
+
+        nc.vector.memset(prm[:], 0.0)
+        nc.vector.memset(bvrow[:], 0.0)
+        nc.vector.memset(ones[:], 1.0)
+        nc.vector.memset(warm[:], 1.0)
+        for i, vec in enumerate((bk, gk, bek, mk, vk)):
+            nc.scalar.dma_start(
+                out=prm[2 * i : 2 * i + 2, :], in_=vec.rearrange("(r p) -> r p", p=P)
+            )
+        nc.scalar.dma_start(out=bvrow[0:1, :], in_=bv.rearrange("(o c) -> o c", o=1))
+        load_x(0, 0)
+        load_w(2, 1, wv[256:384, :])
+        load_x(0, 1)
+        load_w(3, 1, wv[384:512, :])
+        load_w(0, 2, wv[0:256, :])
+        load_w(4, 2, wk)
+        load_x(1, 0)
+        load_x(1, 1)
+        make_identity(nc, ident_b[:])
+        make_identity(nc, ident_f[:])
+        nc.scalar.activation(out=warm[:], in_=warm[:], func=ACT.Sqrt)
+
+        for qt, off, grid, bs in ((q8, 46, 8, 3), (q6, 10, 6, 4), (q3, 1, 3, 8)):
+            nc.vector.tensor_copy(
+                out=qt[:].rearrange("p g (c j) -> p g c j", j=bs),
+                in_=ident_b[:, off : off + grid * grid]
+                .rearrange("p (g c) -> p g c", c=grid)
+                .unsqueeze(3)
+                .to_broadcast([P, grid, grid, bs]),
+            )
+        nc.vector.tensor_copy(
+            out=member[:].rearrange("p (g i) w -> p g i w", i=3),
+            in_=q8[:].unsqueeze(2).to_broadcast([P, 8, 3, 24]),
+        )
+        for qt, grid, bs in ((q6, 6, 4), (q3, 3, 8)):
+            mv = member[:].rearrange("p (g i) w -> p g i w", i=bs)
+            nc.vector.tensor_tensor(
+                out=mv, in0=mv, in1=qt[:].unsqueeze(2).to_broadcast([P, grid, bs, 24]), op=ALU.add
+            )
+        nc.vector.tensor_scalar_add(out=mflat, in0=mflat, scalar1=ident_f[:, 0:1])
+        nc.vector.memset(mtail[:], 0.0)
+        nc.vector.tensor_copy(out=mtail[:, 64:128], in_=mflat[:, 512:576])
+        nc.vector.memset(wloc[:, 0:1], 576.0)
+        nc.vector.memset(wloc[:, 1:10], 64.0)
+        nc.vector.memset(wloc[:, 10:46], 16.0)
+        nc.vector.memset(wloc[:, 46:110], 9.0)
+        nc.vector.reciprocal(out=wloc[:], in_=wloc[:])
+        nc.vector.tensor_mul(out=rtmp[:], in0=ident_f[:, 0:NLOC], in1=wloc[:])
+        nc.vector.tensor_reduce(out=rs[:], in_=rtmp[:], axis=AX.X, op=ALU.add)
+        nc.vector.memset(sums[:, :, :, NLOC:P], 0.0)
+
+        pbv = psum.tile([P, 512], F32, tag="T1")
+        nc.tensor.matmul(out=pbv[:], lhsT=ones[:], rhs=bvrow[:], start=True, stop=True)
+        pprm = psum.tile([P, P], BF16, tag="B1")
+        nc.tensor.transpose(out=pprm[:], in_=prm[:], identity=ident_b[:])
+        pmem = psum.tile([P, 5, P], BF16, tag="B0")
+        for m in range(4):
+            nc.tensor.transpose(
+                out=pmem[:, m, :], in_=mflat[:, P * m : P * m + P], identity=ident_b[:]
+            )
+        nc.tensor.transpose(out=pmem[:, 4, :], in_=mtail[:], identity=ident_b[:])
+        nc.scalar.copy(out=bvb[:], in_=pbv[:])
+        nc.vector.tensor_copy(out=prmt[:], in_=pprm[:, 0:10])
+        nc.vector.tensor_scalar_add(out=sc[:], in0=prmt[:, 8:10], scalar1=EPS)
+        nc.scalar.activation(out=sc[:], in_=sc[:], func=ACT.Sqrt)
+
+        regroup(0, 0, 0, 384, True)
+        regroup(0, 0, 384, 576, False)
+        nc.vector.reciprocal(out=sc[:], in_=sc[:])
+        nc.vector.tensor_mul(out=sc[:], in0=sc[:], in1=prmt[:, 2:4])
+        nc.vector.tensor_sub(out=bi[:], in0=prmt[:, 0:2], in1=prmt[:, 6:8])
+        nc.vector.tensor_mul(out=bi[:], in0=bi[:], in1=sc[:])
+        nc.vector.tensor_add(out=bi[:], in0=bi[:], in1=prmt[:, 4:6])
+        pw2 = weight_transposes(2, "A0")
+        weight_copy(2, pw2, False)
+        quant_x(0, 0, 512)
+        quant_x(0, 512, 576)
+        weight_quant(256, 384)
+        regroup(0, 1, 0, 384, True)
+        regroup(0, 1, 384, 576, False)
+        pw3 = weight_transposes(3, "A1")
+        weight_copy(3, pw3, False)
+        quant_x(1, 0, 512)
+        quant_x(1, 512, 576)
+        weight_quant(384, 512)
+        nc.scalar.copy(out=pmat[:], in_=pmem[:])
+        pw0 = weight_transposes(0, "X0")
+        pw1 = weight_transposes(1, "X1")
+        weight_copy(0, pw0, False)
+        weight_copy(1, pw1, False)
+
+        state = {}
+
+        def begin(b):
+            state["pt", b] = psum.tile([P, 512], F32, tag="T%d" % b, name="pt%d" % b)
+            state["pbv", b] = psum.tile([P, 2, P], F32, tag="B0", name="pb_v%d" % b)
+            state["pbu", b] = psum.tile([P, 2, P], F32, tag="B1", name="pb_u%d" % b)
+            state["r", b] = work.tile([P, 2, NPX], F32, tag="r_sb", name="r_sb%d" % b)
+
+        def v_mx(b, k, bank):
+            pa = psum.tile([P, 512], F32, tag=bank, name="pav%d%d" % (b, k))
+            mx_group(pa[:], 2 + k, NPX * b, 512)
+            mx_group(state["pbv", b][:, k, :], 2 + k, NPX * b + 448, P)
+            state["pav", b, k] = pa
+
+        def v_pool(b, k):
+            pa = state["pav", b, k]
+            pool_pair(
+                pa[:, 0:504].rearrange("p (g i c j) -> p g c i j", i=3, c=8, j=3),
+                sums[:, b, k, 46:102].rearrange("p (g c) -> p g c", c=8),
+                pa[:, 0:480].rearrange("p (g i c j) -> p g c i j", i=4, c=6, j=4),
+                sums[:, b, k, 10:40].rearrange("p (g c) -> p g c", c=6),
+            )
+
+        def v_pool_tail(b):
+            pb_v = state["pbv", b]
+            pool_pair(
+                pb_v[:, :, 56:128].rearrange("p k (i c j) -> p k c i j", i=3, c=8, j=3),
+                sums[:, b, 0:2, 102:110],
+                pb_v[:, :, 32:128].rearrange("p k (i c j) -> p k c i j", i=4, c=6, j=4),
+                sums[:, b, 0:2, 40:46],
+            )
+
+        def u_mx(b, k, bank):
+            pa = psum.tile([P, 512], F32, tag=bank, name="pau%d%d" % (b, k))
+            mx_group(pa[:], 4 + k, NPX * b, 512)
+            mx_group(state["pbu", b][:, k, :], 4 + k, NPX * b + 448, P)
+            r_sb = state["r", b]
+            nc.scalar.activation(
+                out=r_sb[:, k, 0:512], in_=pa[:], func=ACT.Relu,
+                bias=bi[:, k : k + 1], scale=sc[:, k : k + 1],
+            )
+            nc.scalar.activation(
+                out=r_sb[:, k, 512:576], in_=state["pbu", b][:, k, 64:128], func=ACT.Relu,
+                bias=bi[:, k : k + 1], scale=sc[:, k : k + 1],
+            )
+
+        def u_pool(b, k):
+            r_sb = state["r", b]
+            pool_pair(
+                r_sb[:, k, :].rearrange("p (g i c j) -> p g c i j", i=3, c=8, j=3),
+                sums[:, b, 2 + k, 46:110].rearrange("p (g c) -> p g c", c=8),
+                r_sb[:, k, :].rearrange("p (g i c j) -> p g c i j", i=4, c=6, j=4),
+                sums[:, b, 2 + k, 10:46].rearrange("p (g c) -> p g c", c=6),
+            )
+
+        def u_pool_gpsimd(b, k):
+            r_k = state["r", b][:, k, :]
+            add = ALU.add
+            tg = "%d%d" % (b, k)
+            rv3 = r_k.rearrange("p (m j) -> p m j", j=3)
+            t8 = work.tile([P, 192], F32, tag="t8", name="t8_" + tg)
+            nc.gpsimd.tensor_tensor(out=t8[:], in0=rv3[:, :, 0], in1=rv3[:, :, 1], op=add)
+            nc.gpsimd.tensor_tensor(out=t8[:], in0=t8[:], in1=rv3[:, :, 2], op=add)
+            t8v = t8[:].rearrange("p (g i c) -> p g i c", i=3, c=8)
+            u8 = work.tile([P, 8, 8], F32, tag="u8", name="u8_" + tg)
+            nc.gpsimd.tensor_tensor(out=u8[:], in0=t8v[:, :, 0, :], in1=t8v[:, :, 1, :], op=add)
+            nc.gpsimd.tensor_tensor(
+                out=sums[:, b, 2 + k, 46:110].rearrange("p (g c) -> p g c", c=8),
+                in0=u8[:], in1=t8v[:, :, 2, :], op=add,
+            )
+            rv2 = r_k.rearrange("p (m j) -> p m j", j=2)
+            p6 = work.tile([P, 288], F32, tag="p6", name="p6_" + tg)
+            nc.gpsimd.tensor_tensor(out=p6[:], in0=rv2[:, :, 0], in1=rv2[:, :, 1], op=add)
+            p6v = p6[:].rearrange("p (m j) -> p m j", j=2)
+            p6b = work.tile([P, 144], F32, tag="p6b", name="p6b_" + tg)
+            nc.gpsimd.tensor_tensor(out=p6b[:], in0=p6v[:, :, 0], in1=p6v[:, :, 1], op=add)
+            p6bv = p6b[:].rearrange("p (a e c) -> p a e c", e=2, c=6)
+            h6 = work.tile([P, 12, 6], F32, tag="h6", name="h6_" + tg)
+            nc.gpsimd.tensor_tensor(out=h6[:], in0=p6bv[:, :, 0, :], in1=p6bv[:, :, 1, :], op=add)
+            h6v = h6[:].rearrange("p (g a) c -> p g a c", a=2)
+            nc.gpsimd.tensor_tensor(
+                out=sums[:, b, 2 + k, 10:46].rearrange("p (g c) -> p g c", c=6),
+                in0=h6v[:, :, 0, :], in1=h6v[:, :, 1, :], op=add,
+            )
+
+        def px_mx(b, m0, m1, bank):
+            px = psum.tile([P, 2, 256], F32, tag=bank, name="px%d%d" % (b, m0))
+            for m in range(m0, m1):
+                px_group(px[:, m - m0, :], NPX * b + PX_STARTS[m])
+            vsb = vpool.tile([P, 2, 256], F32, tag="vsb", name="vsb%d%d" % (b, m0))
+            nc.scalar.copy(out=vsb[:, 0 : m1 - m0, :], in_=px[:, 0 : m1 - m0, :])
+            state["vsb", b, m0] = vsb
+
+        def px_pool(b, m0, m1):
+            vsb = state["vsb", b, m0]
+            for m in range(m0, m1):
+                nc.tensor.matmul(
+                    out=state["pt", b][:, 0:256], lhsT=pmat[:, m, :], rhs=vsb[:, m - m0, :],
+                    start=(m == 0), stop=(m == 4),
+                )
+
+        rows = sums[:].rearrange("p b q l -> p (b q) l")
+
+        def coarse_grids(q0, q1):
+            half = work.tile([P, q1 - q0, 18], F32, tag="half%d" % q0, name="half%d" % q0)
+            nc.vector.tensor_reduce(
+                out=half[:],
+                in_=rows[:, q0:q1, 10:46].rearrange("p k (m j) -> p k m j", j=2),
+                axis=AX.X, op=ALU.add,
+            )
+            nc.vector.tensor_reduce(
+                out=rows[:, q0:q1, 1:10].rearrange("p k (g c) -> p k g c", c=3),
+                in_=half[:].rearrange("p k (g i c) -> p k g c i", i=2, c=3),
+                axis=AX.X, op=ALU.add,
+            )
+            nc.vector.tensor_reduce(
+                out=rows[:, q0:q1, 0:1], in_=rows[:, q0:q1, 1:10], axis=AX.X, op=ALU.add
+            )
+
+        def value_transposes(b):
+            for k in range(2):
+                nc.tensor.transpose(
+                    out=state["pt", b][:, 256 + P * k : 384 + P * k], in_=sums[:, b, k, :],
+                    identity=ident_f[:],
+                )
+
+        def finish_value(b):
+            vo = work.tile([P, 512], F32, tag="vo", name="vo%d" % b)
+            nc.vector.scalar_tensor_tensor(
+                out=vo[:], in0=state["pt", b][:], scalar=rs[:, 0:1],
+                in1=bvb[:], op0=ALU.mult, op1=ALU.add,
+            )
+            nc.sync.dma_start(out=out_0[b], in_=vo[0:NLOC, :])
+
+        def finish_keys():
+            ko = keep.tile([P, NB, 2, NLOC], F32)
+            nc.gpsimd.tensor_tensor(
+                out=ko[:], in0=sums[:, :, 2:4, 0:NLOC],
+                in1=wloc[:].unsqueeze(1).unsqueeze(1).to_broadcast([P, NB, 2, NLOC]), op=ALU.mult,
+            )
+            for b in range(NB):
+                nc.sync.dma_start(
+                    out=out_1[b].rearrange("(k p) l -> p k l", p=P), in_=ko[:, b, :, :]
+                )
+
+        begin(0)
+        v_mx(0, 0, "A0")
+        pw4 = weight_transposes(4, "T0")
+        pw5 = weight_transposes(5, "T1")
+        weight_copy(4, pw4, False)
+        weight_copy(5, pw5, False)
+        v_mx(0, 1, "A1")
+        v_pool(0, 0)
+        weight_quant(0, 256)
+        regroup(1, 0, 192, 384, "gpsimd")
+        regroup(1, 1, 192, 384, "gpsimd")
+        regroup(1, 0, 384, 576, False)
+        regroup(1, 0, 0, 192, True)
+        weight_quant(512, 768)
+        px_mx(0, 0, 2, "X0")
+        px_mx(0, 2, 4, "X1")
+        quant_x(0, 576, 640)
+        quant_x(0, 640, 1152)
+        v_pool(0, 1)
+        u_mx(0, 0, "A0")
+        px_mx(0, 4, 5, "X0")
+        regroup(1, 1, 384, 576, False)
+        regroup(1, 1, 0, 192, True)
+        px_pool(0, 0, 2)
+        px_pool(0, 2, 4)
+        u_mx(0, 1, "A1")
+        u_pool_gpsimd(0, 0)
+        px_pool(0, 4, 5)
+        v_pool_tail(0)
+        coarse_grids(0, 2)
+        quant_x(1, 576, 640)
+        quant_x(1, 640, 1152)
+        u_pool_gpsimd(0, 1)
+
+        begin(1)
+        v_mx(1, 0, "A0")
+        u_mx(1, 0, "A1")
+        value_transposes(0)
+        v_pool(1, 0)
+        finish_value(0)
+        px_mx(1, 0, 2, "X0")
+        px_mx(1, 2, 4, "X1")
+        v_mx(1, 1, "A1")
+        u_mx(1, 1, "A0")
+        u_pool(1, 0)
+        px_mx(1, 4, 5, "X0")
+        px_pool(1, 0, 2)
+        v_pool(1, 1)
+        v_pool_tail(1)
+        px_pool(1, 2, 4)
+        px_pool(1, 4, 5)
+        u_pool(1, 1)
+        coarse_grids(2, 8)
+        value_transposes(1)
+        finish_keys()
+        finish_value(1)

@@ -15,12 +15,12 @@ AX = mybir.AxisListType
 P = 128
 NB = 2
 NPX = 576
-NX = NB * NPX
+CW = 640
+CV = 512
 CH = 768
 NLOC = 110
 EPS = 1e-5
 FLOPS = 2 * 768 * 1024 * 1152
-PX_STARTS = (0, 128, 256, 384, 448)
 
 
 def tile_afnb_pa_kernel(tc, low_feats, wk, bk, gk, bek, mk, vk, wv, bv, out_0, out_1):
@@ -28,13 +28,14 @@ def tile_afnb_pa_kernel(tc, low_feats, wk, bk, gk, bek, mk, vk, wv, bv, out_0, o
     with ExitStack() as ctx:
         keep = ctx.enter_context(tc.tile_pool(name="keep", bufs=1))
         work = ctx.enter_context(tc.tile_pool(name="work", bufs=2))
-        vpool = ctx.enter_context(tc.tile_pool(name="vpool", bufs=3))
         psum = ctx.enter_context(tc.psum_pool(name="psum", bufs=1))
         ctx.enter_context(tc.manual_schedule())
 
-        prm = keep.tile([P, P], BF16)
-        bvrow = keep.tile([P, 512], BF16)
-        w_sb = keep.tile([P, 6 * 1024], BF16)
+        prm = keep.tile([P, 256], BF16)
+        bvrow = keep.tile([P, CV], BF16)
+        ones = keep.tile([P, P], BF16)
+        w_u = keep.tile([P, 2, 1024], BF16)
+        w_v = keep.tile([P, 4, 1024], BF16)
         xr = []
         for b in range(NB):
             row = []
@@ -48,27 +49,26 @@ def tile_afnb_pa_kernel(tc, low_feats, wk, bk, gk, bek, mk, vk, wv, bv, out_0, o
         q8 = keep.tile([P, 8, 24], BF16)
         q6 = keep.tile([P, 6, 24], BF16)
         q3 = keep.tile([P, 3, 24], BF16)
-        member = keep.tile([P, 24, 24], BF16)
-        mflat = member[:].rearrange("p h w -> p (h w)")
-        mtail = keep.tile([P, P], BF16)
-        pmat = keep.tile([P, 5, P], F32)
-        ones = keep.tile([P, P], BF16)
-        wloc = keep.tile([P, NLOC], F32)
-        rtmp = keep.tile([P, NLOC], F32)
-        rs = keep.tile([P, 1], F32)
-        sums = keep.tile([P, NB, 4, P], F32)
-        prmt = keep.tile([P, 10], F32)
+        muni = keep.tile([P, 384], BF16)
+        pmat = keep.tile([P, 3, P], F32)
+        wloc = keep.tile([P, P], F32)
+        r4 = keep.tile([P, 4], F32)
+        bvb = keep.tile([P, CV], F32)
+        sums8 = keep.tile([P, NB, 2, 64], F32)
+        sums6 = keep.tile([P, NB, 2, 36], F32)
+        half = keep.tile([P, NB, 2, 18], F32)
+        sums3 = keep.tile([P, NB, 2, 9], F32)
+        sums1 = keep.tile([P, NB, 2], F32)
+        prmt = keep.tile([P, 5, 2], F32)
         sc = keep.tile([P, 2], F32)
         bi = keep.tile([P, 2], F32)
-        bvb = keep.tile([P, 512], F32)
-        wf = w_sb[:].bitcast(F32)
         wg = keep.tile([P, 2 * CH * 4], BF16, align_bytes=64)
         wgf = wg[:].bitcast(F32).rearrange("p (g c u) -> p g c u", g=2, u=2)
         wc = keep.tile([P, 2 * CH], U32, align_bytes=64)
         wsc = keep.tile([P, 2 * CH], U8, align_bytes=64)
-        xg = keep.tile([P, 2 * NX * 4], BF16, align_bytes=64)
-        xc = keep.tile([P, 2 * NX], U32, align_bytes=64)
-        xs = keep.tile([P, 2 * NX], U8, align_bytes=64)
+        xg = keep.tile([P, 4 * CW * 4], BF16, align_bytes=64)
+        xc = keep.tile([P, 4 * CW], U32, align_bytes=64)
+        xs = keep.tile([P, 4 * CW], U8, align_bytes=64)
 
         def load_x(b, g):
             nc.sync.dma_start(
@@ -76,34 +76,38 @@ def tile_afnb_pa_kernel(tc, low_feats, wk, bk, gk, bek, mk, vk, wv, bv, out_0, o
                 in_=low_feats[b, 512 * g : 512 * g + 512].rearrange("(q t) h w -> q t (h w)", t=4),
             )
 
-        def load_w(r0, n_blocks, rows):
+        def load_wk(k):
             nc.sync.dma_start(
-                out=w_sb[:, 1024 * r0 : 1024 * (r0 + n_blocks)].rearrange(
-                    "p (r k) -> p r k", k=1024
-                ),
-                in_=rows.rearrange("(r p) k -> p r k", p=P),
+                out=w_u[:, k, :], in_=wk.rearrange("(p k) c -> p k c", k=2)[:, k, :]
             )
 
-        def weight_transposes(r, bank):
-            pw = psum.tile([P, 2, 2, P], F32, tag=bank, name="pw%d" % r)
+        def load_wv(r0):
+            nc.sync.dma_start(
+                out=w_v[:, r0 : r0 + 2, :],
+                in_=wv[P * r0 : P * r0 + 256, :].rearrange("(r p) k -> p r k", p=P),
+            )
+
+        def weight_transposes(words, bank):
+            pw = psum.tile([P, 2, 2, P], F32, tag=bank, name="pw_" + bank)
             for g in range(2):
                 for u in range(2):
-                    c0 = 512 * r + 256 * g
                     nc.tensor.transpose(
-                        out=pw[:, g, u, :], in_=wf[:, c0 + u : c0 + 256 : 2], identity=ident_f[:]
+                        out=pw[:, g, u, :],
+                        in_=words[:, 256 * g + u : 256 * g + 256 : 2],
+                        identity=ident_f[:],
                     )
             return pw
 
-        def weight_copy(r, pw, on_vector):
-            dst = wgf[:, :, P * r : P * r + P, :]
+        def weight_copy(c0, pw, on_vector):
+            dst = wgf[:, :, c0 : c0 + P, :]
             src = pw[:].rearrange("p g u c -> p g c u")
             if on_vector:
                 nc.vector.tensor_copy(out=dst, in_=src)
             else:
                 nc.scalar.copy(out=dst, in_=src)
 
-        def weight_quant(c0, c1):
-            for g in range(2):
+        def weight_quant(c0, c1, gs=(0, 1)):
+            for g in gs:
                 lo = g * CH + c0
                 hi = g * CH + c1
                 nc.vector.quantize_mx(
@@ -112,82 +116,223 @@ def tile_afnb_pa_kernel(tc, low_feats, wk, bk, gk, bek, mk, vk, wv, bv, out_0, o
                     in_=wg[:, 4 * lo : 4 * hi],
                 )
 
-        def regroup(b, g, a0, a1, on_vector):
-            base = g * NX + NPX * b
-            dst = xg[:, 4 * (base + a0) : 4 * (base + a1)].rearrange(
-                "p (c i t) -> p c t i", i=4, t=4
-            )
-            src = xr[b][g][:, :, a0:a1].rearrange("p t (c i) -> p c t i", i=4)
-            if on_vector == "gpsimd":
-                nc.gpsimd.tensor_scalar(
-                    out=dst, in0=src, scalar1=1.0, scalar2=0.0, op0=ALU.mult, op1=ALU.add
+        def xcol(b, g):
+            return (2 * b + g) * CW
+
+        def regroup(b, g, part, copy):
+            base = xcol(b, g)
+            if part == 1:
+                dst = xg[:, 4 * base : 4 * (base + 192)].rearrange(
+                    "p (m c i t) -> p m c t i", m=8, i=4, t=4
                 )
-            elif on_vector:
-                nc.vector.tensor_copy(out=dst, in_=src)
+                src = xr[b][g][:].rearrange("p t (m c i) -> p m c t i", m=8, i=4)[:, :, 6:12, :, :]
+            elif part == 0:
+                dst = xg[:, 4 * (base + 192) : 4 * (base + 384)].rearrange(
+                    "p (q c i t) -> p q c t i", q=4, i=4, t=4
+                )
+                src = xr[b][g][:].rearrange("p t (q c i) -> p q c t i", q=4, i=4)[:, :, 12:24, :, :]
             else:
-                nc.scalar.copy(out=dst, in_=src)
+                w = part - 2
+                dst = xg[:, 4 * (base + 384) : 4 * (base + 576)].rearrange(
+                    "p (q w c i t) -> p q w c t i", q=4, w=2, i=4, t=4
+                )[:, :, w, :, :, :]
+                src = xr[b][g][:].rearrange("p t (q c i) -> p q c t i", q=4, i=4)[
+                    :, :, 30 * w : 30 * w + 6, :, :
+                ]
+            copy(out=dst, in_=src)
 
-        def quant_x(g, lo, hi):
-            lo = g * NX + lo
-            hi = g * NX + hi
-            nc.vector.quantize_mx(
-                out=xc[:, lo:hi].bitcast(FP8X4),
-                scales=xs[:, lo:hi],
-                in_=xg[:, 4 * lo : 4 * hi],
-            )
+        def regroup_vector(b, g, parts=(1, 2)):
+            for part in parts:
+                regroup(b, g, part, nc.vector.tensor_copy)
 
-        def mx_group(out, blk, lo, n):
-            for g in range(2):
-                w0 = g * CH + P * blk
-                x0 = g * NX + lo
+        def regroup_scalar(b, g, parts=(0, 3)):
+            for part in parts:
+                regroup(b, g, part, nc.scalar.copy)
+
+        def quant_x(b, g):
+            for lo, hi in ((0, 512), (512, 640)):
+                lo += xcol(b, g)
+                hi += xcol(b, g)
+                nc.vector.quantize_mx(
+                    out=xc[:, lo:hi].bitcast(FP8X4),
+                    scales=xs[:, lo:hi],
+                    in_=xg[:, 4 * lo : 4 * hi],
+                )
+
+        state = {}
+
+        def u_open(b):
+            for k in range(2):
+                state["pu", b, k] = psum.tile([P, 384], F32, tag="U%d" % k, name="pu%d_%d" % (k, b))
+            state["pu", b, 2] = psum.tile([P, 2, 256], F32, tag="U2", name="pu2_%d" % b)
+
+        def u_win(b, k, win, gs=(0, 1)):
+            w0 = CV + P * k
+            out, lo, n = (
+                (state["pu", b, k][:, 0:256], 0, 256),
+                (state["pu", b, k][:, 256:384], 256, 128),
+                (state["pu", b, 2][:, k, :], 384, 256),
+            )[win]
+            for g in gs:
+                x0 = xcol(b, g) + lo
                 nc.tensor.matmul_mx(
                     out=out,
-                    lhsT=wc[:, w0 : w0 + P].bitcast(FP8X4),
-                    lhsT_scale=wsc[:, w0 : w0 + P],
+                    lhsT=wc[:, g * CH + w0 : g * CH + w0 + P].bitcast(FP8X4),
+                    lhsT_scale=wsc[:, g * CH + w0 : g * CH + w0 + P],
                     rhs=xc[:, x0 : x0 + n].bitcast(FP8X4),
                     rhs_scale=xs[:, x0 : x0 + n],
                     start=(g == 0),
                     stop=(g == 1),
                 )
 
-        def px_group(out, lo):
-            for g in range(2):
-                x0 = g * NX + lo
-                nc.tensor.matmul_mx(
-                    out=out,
-                    lhsT=xc[:, x0 : x0 + P].bitcast(FP8X4),
-                    lhsT_scale=xs[:, x0 : x0 + P],
-                    rhs=wc[:, g * CH : g * CH + 256].bitcast(FP8X4),
-                    rhs_scale=wsc[:, g * CH : g * CH + 256],
-                    start=(g == 0),
-                    stop=(g == 1),
+        def u_mx(b, k):
+            for win in range(3):
+                u_win(b, k, win)
+
+        def u_relu(b, k):
+            if k == 0:
+                state["r", b] = work.tile([P, 2, NPX], F32, tag="r_sb", name="r_sb%d" % b)
+            r_k = state["r", b][:, k, :]
+            pu = state["pu", b, k]
+            pu2 = state["pu", b, 2]
+            for dst, src in (
+                (
+                    r_k.rearrange("p (m r w) -> p m r w", m=8, r=3)[:, :, 1, :],
+                    pu[:, 0:192].rearrange("p (m w) -> p m w", m=8),
+                ),
+                (
+                    r_k.rearrange("p (q v) -> p q v", q=4)[:, :, 48:96],
+                    pu[:, 192:384].rearrange("p (q v) -> p q v", q=4),
+                ),
+                (
+                    r_k.rearrange("p (q r w) -> p q r w", q=4, r=6)[:, :, 0:6:5, :],
+                    pu2[:, k, 0:192].rearrange("p (q r w) -> p q r w", q=4, r=2),
+                ),
+            ):
+                nc.scalar.activation(
+                    out=dst, in_=src, func=ACT.Relu, bias=bi[:, k : k + 1], scale=sc[:, k : k + 1]
                 )
 
-        def pool_pair(src8, dst8, src6, dst6):
-            nc.vector.tensor_reduce(out=dst8, in_=src8, axis=AX.XY, op=ALU.add)
-            nc.vector.tensor_reduce(out=dst6, in_=src6, axis=AX.XY, op=ALU.add)
+        V_PASSES = {"X": (0, 384), "Y": (128, 512), "Z": (256,)}
 
-        nc.vector.memset(prm[:], 0.0)
-        nc.vector.memset(bvrow[:], 0.0)
-        nc.vector.memset(ones[:], 1.0)
-        nc.vector.memset(warm[:], 1.0)
-        for i, vec in enumerate((bk, gk, bek, mk, vk)):
-            nc.scalar.dma_start(
-                out=prm[2 * i : 2 * i + 2, :], in_=vec.rearrange("(r p) -> r p", p=P)
+        def v_mx(b, bank, g):
+            if g == 0:
+                state[bank, b] = psum.tile([P, CV], F32, tag=bank, name="pv%s%d" % (bank, b))
+            offs = V_PASSES[bank]
+            for i, off in enumerate(offs):
+                x0 = xcol(b, g) + off
+                nc.tensor.matmul_mx(
+                    out=state[bank, b][:],
+                    lhsT=xc[:, x0 : x0 + P].bitcast(FP8X4),
+                    lhsT_scale=xs[:, x0 : x0 + P],
+                    rhs=wc[:, g * CH : g * CH + CV].bitcast(FP8X4),
+                    rhs_scale=wsc[:, g * CH : g * CH + CV],
+                    start=(g == 0 and i == 0),
+                    stop=(g == 1 and i == len(offs) - 1),
+                )
+
+        def v_copy(b, bank, on_vector):
+            vsb = work.tile([P, CV], F32, tag="v" + bank, name="vsb%s%d" % (bank, b))
+            state["v" + bank, b] = vsb
+            if on_vector:
+                nc.vector.tensor_copy(out=vsb[:], in_=state[bank, b][:])
+            else:
+                nc.scalar.copy(out=vsb[:], in_=state[bank, b][:])
+
+        def v_pool(b, bank):
+            for h in range(2):
+                if bank == "X":
+                    state["pt", b, h] = psum.tile([P, 256], F32, tag="T%d" % h, name="pt%d%d" % (b, h))
+                nc.tensor.matmul(
+                    out=state["pt", b, h][:], lhsT=pmat[:, "XYZ".index(bank), :],
+                    rhs=state["v" + bank, b][:, 256 * h : 256 * h + 256],
+                    start=(bank == "X"), stop=(bank == "Z"),
+                )
+
+        def finish_value(b, h):
+            vo = work.tile([P, 256], F32, tag="vo%d" % h, name="vo%d%d" % (b, h))
+            nc.vector.tensor_tensor(
+                out=vo[:], in0=state["pt", b, h][:], in1=bvb[:, 256 * h : 256 * h + 256], op=ALU.add
             )
+            nc.sync.dma_start(out=out_0[b, :, 256 * h : 256 * h + 256], in_=vo[0:NLOC, :])
+
+        def u_pool8(b, k0, k1):
+            nc.vector.tensor_reduce(
+                out=sums8[:, b, k0:k1, :].rearrange("p k (g c) -> p (k g) c", c=8),
+                in_=state["r", b][:, k0:k1, :].rearrange(
+                    "p k (g i c j) -> p (k g) c i j", i=3, c=8, j=3
+                ),
+                axis=AX.XY, op=ALU.add,
+            )
+
+        def u_pool6(b, k0, k1):
+            nc.vector.tensor_reduce(
+                out=sums6[:, b, k0:k1, :].rearrange("p k (g c) -> p (k g) c", c=6),
+                in_=state["r", b][:, k0:k1, :].rearrange(
+                    "p k (g i c j) -> p (k g) c i j", i=4, c=6, j=4
+                ),
+                axis=AX.XY, op=ALU.add,
+            )
+
+        def u_pool31(b):
+            nc.vector.tensor_reduce(
+                out=half[:, b, :, :],
+                in_=sums6[:, b, :, :].rearrange("p k (m j) -> p k m j", j=2),
+                axis=AX.X, op=ALU.add,
+            )
+            nc.vector.tensor_reduce(
+                out=sums1[:, b, :], in_=sums6[:, b, :, :], axis=AX.X, op=ALU.add
+            )
+            nc.vector.tensor_reduce(
+                out=sums3[:, b, :, :].rearrange("p k (g c) -> p (k g) c", c=3),
+                in_=half[:, b, :, :].rearrange("p k (g i c) -> p (k g) c i", i=2, c=3),
+                axis=AX.X, op=ALU.add,
+            )
+
+        def scale_keys(b, which):
+            if which == 8:
+                state["ko", b] = work.tile([P, 2, NLOC], F32, tag="ko", name="ko%d" % b)
+            ko = state["ko", b]
+            for dst, src, count in (
+                ((ko[:, :, 46:110], sums8[:, b, :, :], 9),)
+                if which == 8
+                else (
+                    (ko[:, :, 10:46], sums6[:, b, :, :], 16),
+                    (ko[:, :, 1:10], sums3[:, b, :, :], 64),
+                    (ko[:, :, 0], sums1[:, b, :], 576),
+                )
+            ):
+                nc.gpsimd.tensor_scalar(
+                    out=dst, in0=src, scalar1=1.0 / count, scalar2=0.0, op0=ALU.mult, op1=ALU.add
+                )
+
+        def store_keys(b):
+            nc.sync.dma_start(out=out_1[b].rearrange("(p k) l -> p k l", k=2), in_=state["ko", b][:])
+
+        nc.vector.memset(bvrow[:], 0.0)
+        nc.vector.memset(warm[:], 1.0)
+        nc.vector.memset(ones[:], 1.0)
+        nc.vector.memset(prm[:], 0.0)
+        load_wk(0)
         nc.scalar.dma_start(out=bvrow[0:1, :], in_=bv.rearrange("(o c) -> o c", o=1))
+        load_wk(1)
+        load_wv(0)
         load_x(0, 0)
-        load_w(2, 1, wv[256:384, :])
+        load_wv(2)
         load_x(0, 1)
-        load_w(3, 1, wv[384:512, :])
-        load_w(0, 2, wv[0:256, :])
-        load_w(4, 2, wk)
+        for i, vec in enumerate((bk, gk, bek, mk, vk)):
+            nc.sync.dma_start(out=prm[i : i + 1, :], in_=vec.rearrange("(o c) -> o c", o=1))
         load_x(1, 0)
         load_x(1, 1)
+        nc.scalar.activation(out=warm[:], in_=warm[:], func=ACT.Sqrt)
         make_identity(nc, ident_b[:])
         make_identity(nc, ident_f[:])
-        nc.scalar.activation(out=warm[:], in_=warm[:], func=ACT.Sqrt)
-
+        nc.gpsimd.memset(r4[:, 0:1], 576.0)
+        nc.gpsimd.memset(r4[:, 1:2], 64.0)
+        nc.gpsimd.memset(r4[:, 2:3], 16.0)
+        nc.gpsimd.memset(r4[:, 3:4], 9.0)
+        nc.gpsimd.memset(wloc[:], 1.0)
+        nc.gpsimd.memset(xg[:].rearrange("p (a c) -> p a c", a=4)[:, :, 4 * NPX : 4 * CW], 0.0)
         for qt, off, grid, bs in ((q8, 46, 8, 3), (q6, 10, 6, 4), (q3, 1, 3, 8)):
             nc.vector.tensor_copy(
                 out=qt[:].rearrange("p g (c j) -> p g c j", j=bs),
@@ -196,265 +341,137 @@ def tile_afnb_pa_kernel(tc, low_feats, wk, bk, gk, bek, mk, vk, wv, bv, out_0, o
                 .unsqueeze(3)
                 .to_broadcast([P, grid, grid, bs]),
             )
-        nc.vector.tensor_copy(
-            out=member[:].rearrange("p (g i) w -> p g i w", i=3),
-            in_=q8[:].unsqueeze(2).to_broadcast([P, 8, 3, 24]),
+        nc.vector.reciprocal(out=r4[:], in_=r4[:])
+        for i, (lo, hi) in enumerate(((0, 1), (1, 10), (10, 46), (46, P))):
+            nc.gpsimd.tensor_scalar(
+                out=wloc[:, lo:hi], in0=wloc[:, lo:hi], scalar1=r4[:, i : i + 1], scalar2=0.0,
+                op0=ALU.mult, op1=ALU.add,
+            )
+        q6r = q6[:].rearrange("p (g i) w -> p g i w", i=2)
+        nc.vector.tensor_scalar_add(out=q3[:], in0=q3[:], scalar1=ident_f[:, 0:1])
+        nc.vector.tensor_tensor(
+            out=q6r, in0=q6r, in1=q3[:].unsqueeze(2).to_broadcast([P, 3, 2, 24]), op=ALU.add
         )
-        for qt, grid, bs in ((q6, 6, 4), (q3, 3, 8)):
-            mv = member[:].rearrange("p (g i) w -> p g i w", i=bs)
+        m12 = muni[:, 0:192].rearrange("p (h a v) -> p h a v", h=2, a=2)
+        q8a = q8[:].rearrange("p (h a b) w -> p h a (b w)", h=2, a=2)
+        q6h = q6[:].rearrange("p (h r) w -> p h (r w)", h=2)
+        for a in range(2):
             nc.vector.tensor_tensor(
-                out=mv, in0=mv, in1=qt[:].unsqueeze(2).to_broadcast([P, grid, bs, 24]), op=ALU.add
+                out=m12[:, :, a, :], in0=q8a[:, :, a, :], in1=q6h[:, :, 24 * a : 24 * a + 48], op=ALU.add
             )
-        nc.vector.tensor_scalar_add(out=mflat, in0=mflat, scalar1=ident_f[:, 0:1])
-        nc.vector.memset(mtail[:], 0.0)
-        nc.vector.tensor_copy(out=mtail[:, 64:128], in_=mflat[:, 512:576])
-        nc.vector.memset(wloc[:, 0:1], 576.0)
-        nc.vector.memset(wloc[:, 1:10], 64.0)
-        nc.vector.memset(wloc[:, 10:46], 16.0)
-        nc.vector.memset(wloc[:, 46:110], 9.0)
-        nc.vector.reciprocal(out=wloc[:], in_=wloc[:])
-        nc.vector.tensor_mul(out=rtmp[:], in0=ident_f[:, 0:NLOC], in1=wloc[:])
-        nc.vector.tensor_reduce(out=rs[:], in_=rtmp[:], axis=AX.X, op=ALU.add)
-        nc.vector.memset(sums[:, :, :, NLOC:P], 0.0)
-
-        pbv = psum.tile([P, 512], F32, tag="T1")
+        m0 = muni[:, 192:384].rearrange("p (a b w) -> p a b w", a=4, b=2)
+        q8b = q8[:].rearrange("p (a b) w -> p a b w", a=4)
+        for h in range(2):
+            nc.vector.tensor_tensor(
+                out=m0[:, 2 * h : 2 * h + 2, :, :],
+                in0=q8b[:, 2 * h : 2 * h + 2, :, :],
+                in1=q6[:, 3 * h : 3 * h + 3 : 2, :].unsqueeze(2).to_broadcast([P, 2, 2, 24]),
+                op=ALU.add,
+            )
+        pbv = psum.tile([P, CV], F32, tag="T0", name="pbv")
         nc.tensor.matmul(out=pbv[:], lhsT=ones[:], rhs=bvrow[:], start=True, stop=True)
-        pprm = psum.tile([P, P], BF16, tag="B1")
-        nc.tensor.transpose(out=pprm[:], in_=prm[:], identity=ident_b[:])
-        pmem = psum.tile([P, 5, P], BF16, tag="B0")
-        for m in range(4):
+        aux = psum.tile([P, 5, P], BF16, tag="T1", name="aux")
+        for j in range(3):
             nc.tensor.transpose(
-                out=pmem[:, m, :], in_=mflat[:, P * m : P * m + P], identity=ident_b[:]
+                out=aux[:, j, :], in_=muni[:, P * j : P * j + P], identity=ident_b[:]
             )
-        nc.tensor.transpose(out=pmem[:, 4, :], in_=mtail[:], identity=ident_b[:])
         nc.scalar.copy(out=bvb[:], in_=pbv[:])
-        nc.vector.tensor_copy(out=prmt[:], in_=pprm[:, 0:10])
-        nc.vector.tensor_scalar_add(out=sc[:], in0=prmt[:, 8:10], scalar1=EPS)
-        nc.scalar.activation(out=sc[:], in_=sc[:], func=ACT.Sqrt)
-
-        regroup(0, 0, 0, 384, True)
-        regroup(0, 0, 384, 576, False)
-        nc.vector.reciprocal(out=sc[:], in_=sc[:])
-        nc.vector.tensor_mul(out=sc[:], in0=sc[:], in1=prmt[:, 2:4])
-        nc.vector.tensor_sub(out=bi[:], in0=prmt[:, 0:2], in1=prmt[:, 6:8])
-        nc.vector.tensor_mul(out=bi[:], in0=bi[:], in1=sc[:])
-        nc.vector.tensor_add(out=bi[:], in0=bi[:], in1=prmt[:, 4:6])
-        pw2 = weight_transposes(2, "A0")
-        weight_copy(2, pw2, False)
-        quant_x(0, 0, 512)
-        quant_x(0, 512, 576)
-        weight_quant(256, 384)
-        regroup(0, 1, 0, 384, True)
-        regroup(0, 1, 384, 576, False)
-        pw3 = weight_transposes(3, "A1")
-        weight_copy(3, pw3, False)
-        quant_x(1, 0, 512)
-        quant_x(1, 512, 576)
-        weight_quant(384, 512)
-        nc.scalar.copy(out=pmat[:], in_=pmem[:])
-        pw0 = weight_transposes(0, "X0")
-        pw1 = weight_transposes(1, "X1")
+        pu0 = weight_transposes(w_u[:, 0, :].bitcast(F32), "U0")
+        pu1 = weight_transposes(w_u[:, 1, :].bitcast(F32), "U1")
+        weight_copy(CV, pu0, False)
+        weight_copy(CV + P, pu1, True)
+        pw0 = weight_transposes(w_v[:, 0, :].bitcast(F32), "X")
+        pw1 = weight_transposes(w_v[:, 1, :].bitcast(F32), "Y")
         weight_copy(0, pw0, False)
-        weight_copy(1, pw1, False)
-
-        state = {}
-
-        def begin(b):
-            state["pt", b] = psum.tile([P, 512], F32, tag="T%d" % b, name="pt%d" % b)
-            state["pbv", b] = psum.tile([P, 2, P], F32, tag="B0", name="pb_v%d" % b)
-            state["pbu", b] = psum.tile([P, 2, P], F32, tag="B1", name="pb_u%d" % b)
-            state["r", b] = work.tile([P, 2, NPX], F32, tag="r_sb", name="r_sb%d" % b)
-
-        def v_mx(b, k, bank):
-            pa = psum.tile([P, 512], F32, tag=bank, name="pav%d%d" % (b, k))
-            mx_group(pa[:], 2 + k, NPX * b, 512)
-            mx_group(state["pbv", b][:, k, :], 2 + k, NPX * b + 448, P)
-            state["pav", b, k] = pa
-
-        def v_pool(b, k):
-            pa = state["pav", b, k]
-            pool_pair(
-                pa[:, 0:504].rearrange("p (g i c j) -> p g c i j", i=3, c=8, j=3),
-                sums[:, b, k, 46:102].rearrange("p (g c) -> p g c", c=8),
-                pa[:, 0:480].rearrange("p (g i c j) -> p g c i j", i=4, c=6, j=4),
-                sums[:, b, k, 10:40].rearrange("p (g c) -> p g c", c=6),
-            )
-
-        def v_pool_tail(b):
-            pb_v = state["pbv", b]
-            pool_pair(
-                pb_v[:, :, 56:128].rearrange("p k (i c j) -> p k c i j", i=3, c=8, j=3),
-                sums[:, b, 0:2, 102:110],
-                pb_v[:, :, 32:128].rearrange("p k (i c j) -> p k c i j", i=4, c=6, j=4),
-                sums[:, b, 0:2, 40:46],
-            )
-
-        def u_mx(b, k, bank):
-            pa = psum.tile([P, 512], F32, tag=bank, name="pau%d%d" % (b, k))
-            mx_group(pa[:], 4 + k, NPX * b, 512)
-            mx_group(state["pbu", b][:, k, :], 4 + k, NPX * b + 448, P)
-            r_sb = state["r", b]
-            nc.scalar.activation(
-                out=r_sb[:, k, 0:512], in_=pa[:], func=ACT.Relu,
-                bias=bi[:, k : k + 1], scale=sc[:, k : k + 1],
-            )
-            nc.scalar.activation(
-                out=r_sb[:, k, 512:576], in_=state["pbu", b][:, k, 64:128], func=ACT.Relu,
-                bias=bi[:, k : k + 1], scale=sc[:, k : k + 1],
-            )
-
-        def u_pool(b, k):
-            r_sb = state["r", b]
-            pool_pair(
-                r_sb[:, k, :].rearrange("p (g i c j) -> p g c i j", i=3, c=8, j=3),
-                sums[:, b, 2 + k, 46:110].rearrange("p (g c) -> p g c", c=8),
-                r_sb[:, k, :].rearrange("p (g i c j) -> p g c i j", i=4, c=6, j=4),
-                sums[:, b, 2 + k, 10:46].rearrange("p (g c) -> p g c", c=6),
-            )
-
-        def u_pool_gpsimd(b, k):
-            r_k = state["r", b][:, k, :]
-            add = ALU.add
-            tg = "%d%d" % (b, k)
-            rv3 = r_k.rearrange("p (m j) -> p m j", j=3)
-            t8 = work.tile([P, 192], F32, tag="t8", name="t8_" + tg)
-            nc.gpsimd.tensor_tensor(out=t8[:], in0=rv3[:, :, 0], in1=rv3[:, :, 1], op=add)
-            nc.gpsimd.tensor_tensor(out=t8[:], in0=t8[:], in1=rv3[:, :, 2], op=add)
-            t8v = t8[:].rearrange("p (g i c) -> p g i c", i=3, c=8)
-            u8 = work.tile([P, 8, 8], F32, tag="u8", name="u8_" + tg)
-            nc.gpsimd.tensor_tensor(out=u8[:], in0=t8v[:, :, 0, :], in1=t8v[:, :, 1, :], op=add)
-            nc.gpsimd.tensor_tensor(
-                out=sums[:, b, 2 + k, 46:110].rearrange("p (g c) -> p g c", c=8),
-                in0=u8[:], in1=t8v[:, :, 2, :], op=add,
-            )
-            rv2 = r_k.rearrange("p (m j) -> p m j", j=2)
-            p6 = work.tile([P, 288], F32, tag="p6", name="p6_" + tg)
-            nc.gpsimd.tensor_tensor(out=p6[:], in0=rv2[:, :, 0], in1=rv2[:, :, 1], op=add)
-            p6v = p6[:].rearrange("p (m j) -> p m j", j=2)
-            p6b = work.tile([P, 144], F32, tag="p6b", name="p6b_" + tg)
-            nc.gpsimd.tensor_tensor(out=p6b[:], in0=p6v[:, :, 0], in1=p6v[:, :, 1], op=add)
-            p6bv = p6b[:].rearrange("p (a e c) -> p a e c", e=2, c=6)
-            h6 = work.tile([P, 12, 6], F32, tag="h6", name="h6_" + tg)
-            nc.gpsimd.tensor_tensor(out=h6[:], in0=p6bv[:, :, 0, :], in1=p6bv[:, :, 1, :], op=add)
-            h6v = h6[:].rearrange("p (g a) c -> p g a c", a=2)
-            nc.gpsimd.tensor_tensor(
-                out=sums[:, b, 2 + k, 10:46].rearrange("p (g c) -> p g c", c=6),
-                in0=h6v[:, :, 0, :], in1=h6v[:, :, 1, :], op=add,
-            )
-
-        def px_mx(b, m0, m1, bank):
-            px = psum.tile([P, 2, 256], F32, tag=bank, name="px%d%d" % (b, m0))
-            for m in range(m0, m1):
-                px_group(px[:, m - m0, :], NPX * b + PX_STARTS[m])
-            vsb = vpool.tile([P, 2, 256], F32, tag="vsb", name="vsb%d%d" % (b, m0))
-            nc.scalar.copy(out=vsb[:, 0 : m1 - m0, :], in_=px[:, 0 : m1 - m0, :])
-            state["vsb", b, m0] = vsb
-
-        def px_pool(b, m0, m1):
-            vsb = state["vsb", b, m0]
-            for m in range(m0, m1):
-                nc.tensor.matmul(
-                    out=state["pt", b][:, 0:256], lhsT=pmat[:, m, :], rhs=vsb[:, m - m0, :],
-                    start=(m == 0), stop=(m == 4),
-                )
-
-        rows = sums[:].rearrange("p b q l -> p (b q) l")
-
-        def coarse_grids(q0, q1):
-            half = work.tile([P, q1 - q0, 18], F32, tag="half%d" % q0, name="half%d" % q0)
-            nc.vector.tensor_reduce(
-                out=half[:],
-                in_=rows[:, q0:q1, 10:46].rearrange("p k (m j) -> p k m j", j=2),
-                axis=AX.X, op=ALU.add,
-            )
-            nc.vector.tensor_reduce(
-                out=rows[:, q0:q1, 1:10].rearrange("p k (g c) -> p k g c", c=3),
-                in_=half[:].rearrange("p k (g i c) -> p k g c i", i=2, c=3),
-                axis=AX.X, op=ALU.add,
-            )
-            nc.vector.tensor_reduce(
-                out=rows[:, q0:q1, 0:1], in_=rows[:, q0:q1, 1:10], axis=AX.X, op=ALU.add
-            )
-
-        def value_transposes(b):
-            for k in range(2):
-                nc.tensor.transpose(
-                    out=state["pt", b][:, 256 + P * k : 384 + P * k], in_=sums[:, b, k, :],
-                    identity=ident_f[:],
-                )
-
-        def finish_value(b):
-            vo = work.tile([P, 512], F32, tag="vo", name="vo%d" % b)
-            nc.vector.scalar_tensor_tensor(
-                out=vo[:], in0=state["pt", b][:], scalar=rs[:, 0:1],
-                in1=bvb[:], op0=ALU.mult, op1=ALU.add,
-            )
-            nc.sync.dma_start(out=out_0[b], in_=vo[0:NLOC, :])
-
-        def finish_keys():
-            ko = keep.tile([P, NB, 2, NLOC], F32)
-            nc.gpsimd.tensor_tensor(
-                out=ko[:], in0=sums[:, :, 2:4, 0:NLOC],
-                in1=wloc[:].unsqueeze(1).unsqueeze(1).to_broadcast([P, NB, 2, NLOC]), op=ALU.mult,
-            )
-            for b in range(NB):
-                nc.sync.dma_start(
-                    out=out_1[b].rearrange("(k p) l -> p k l", p=P), in_=ko[:, b, :, :]
-                )
-
-        begin(0)
-        v_mx(0, 0, "A0")
-        pw4 = weight_transposes(4, "T0")
-        pw5 = weight_transposes(5, "T1")
-        weight_copy(4, pw4, False)
-        weight_copy(5, pw5, False)
-        v_mx(0, 1, "A1")
-        v_pool(0, 0)
-        weight_quant(0, 256)
-        regroup(1, 0, 192, 384, "gpsimd")
-        regroup(1, 1, 192, 384, "gpsimd")
-        regroup(1, 0, 384, 576, False)
-        regroup(1, 0, 0, 192, True)
-        weight_quant(512, 768)
-        px_mx(0, 0, 2, "X0")
-        px_mx(0, 2, 4, "X1")
-        quant_x(0, 576, 640)
-        quant_x(0, 640, 1152)
-        v_pool(0, 1)
-        u_mx(0, 0, "A0")
-        px_mx(0, 4, 5, "X0")
-        regroup(1, 1, 384, 576, False)
-        regroup(1, 1, 0, 192, True)
-        px_pool(0, 0, 2)
-        px_pool(0, 2, 4)
-        u_mx(0, 1, "A1")
-        u_pool_gpsimd(0, 0)
-        px_pool(0, 4, 5)
-        v_pool_tail(0)
-        coarse_grids(0, 2)
-        quant_x(1, 576, 640)
-        quant_x(1, 640, 1152)
-        u_pool_gpsimd(0, 1)
-
-        begin(1)
-        v_mx(1, 0, "A0")
-        u_mx(1, 0, "A1")
-        value_transposes(0)
-        v_pool(1, 0)
-        finish_value(0)
-        px_mx(1, 0, 2, "X0")
-        px_mx(1, 2, 4, "X1")
-        v_mx(1, 1, "A1")
-        u_mx(1, 1, "A0")
-        u_pool(1, 0)
-        px_mx(1, 4, 5, "X0")
-        px_pool(1, 0, 2)
-        v_pool(1, 1)
-        v_pool_tail(1)
-        px_pool(1, 2, 4)
-        px_pool(1, 4, 5)
-        u_pool(1, 1)
-        coarse_grids(2, 8)
-        value_transposes(1)
-        finish_keys()
-        finish_value(1)
+        weight_quant(CV, CH)
+        regroup_vector(0, 0)
+        regroup_scalar(0, 0)
+        weight_copy(P, pw1, True)
+        quant_x(0, 0)
+        pw2 = weight_transposes(w_v[:, 2, :].bitcast(F32), "Z")
+        pw3 = weight_transposes(w_v[:, 3, :].bitcast(F32), "U2")
+        weight_copy(2 * P, pw2, False)
+        weight_copy(3 * P, pw3, False)
+        weight_quant(0, CV, (0,))
+        u_open(0)
+        u_win(0, 0, 0, (0,))
+        u_win(0, 1, 0, (0,))
+        u_win(0, 0, 2, (0,))
+        for k in range(2):
+            nc.tensor.transpose(out=aux[:, 3 + k, :], in_=prm[:, k:256:2], identity=ident_b[:])
+        nc.vector.tensor_copy(out=prmt[:].rearrange("p v k -> p k v"), in_=aux[:, 3:5, 0:5])
+        nc.vector.tensor_scalar_add(out=sc[:], in0=prmt[:, 4, :], scalar1=EPS)
+        weight_quant(0, CV, (1,))
+        v_mx(0, "X", 0)
+        v_mx(0, "Y", 0)
+        v_mx(0, "Z", 0)
+        regroup_vector(0, 1)
+        regroup_scalar(0, 1)
+        nc.scalar.activation(out=sc[:], in_=sc[:], func=ACT.Sqrt)
+        quant_x(0, 1)
+        nc.vector.reciprocal(out=sc[:], in_=sc[:])
+        nc.gpsimd.tensor_tensor(out=bi[:], in0=prmt[:, 0, :], in1=prmt[:, 3, :], op=ALU.subtract)
+        nc.gpsimd.tensor_tensor(out=sc[:], in0=sc[:], in1=prmt[:, 1, :], op=ALU.mult)
+        nc.gpsimd.tensor_tensor(out=bi[:], in0=bi[:], in1=sc[:], op=ALU.mult)
+        nc.gpsimd.tensor_tensor(out=bi[:], in0=bi[:], in1=prmt[:, 2, :], op=ALU.add)
+        v_mx(0, "X", 1)
+        u_win(0, 0, 0, (1,))
+        u_win(0, 1, 0, (1,))
+        u_win(0, 0, 2, (1,))
+        u_win(0, 0, 1)
+        u_win(0, 1, 1)
+        u_win(0, 1, 2)
+        v_mx(0, "Y", 1)
+        v_mx(0, "Z", 1)
+        regroup_vector(1, 0)
+        regroup_scalar(1, 0)
+        quant_x(1, 0)
+        v_copy(0, "X", False)
+        u_relu(0, 0)
+        regroup_vector(1, 1)
+        regroup_scalar(1, 1)
+        nc.vector.tensor_tensor(
+            out=pmat[:], in0=aux[:, 0:3, :], in1=wloc[:].unsqueeze(1).to_broadcast([P, 3, P]), op=ALU.mult
+        )
+        quant_x(1, 1)
+        v_copy(0, "Y", False)
+        v_copy(0, "Z", False)
+        u_relu(0, 1)
+        v_pool(0, "X")
+        v_mx(1, "X", 0)
+        v_mx(1, "Y", 0)
+        v_mx(1, "Z", 0)
+        v_mx(1, "X", 1)
+        v_copy(1, "X", False)
+        v_mx(1, "Y", 1)
+        v_copy(1, "Y", False)
+        u_pool8(0, 0, 2)
+        u_pool6(0, 0, 2)
+        u_pool31(0)
+        scale_keys(0, 8)
+        scale_keys(0, 6)
+        store_keys(0)
+        u_open(1)
+        u_mx(1, 0)
+        u_relu(1, 0)
+        u_mx(1, 1)
+        u_relu(1, 1)
+        v_mx(1, "Z", 1)
+        v_copy(1, "Z", False)
+        v_pool(0, "Y")
+        v_pool(0, "Z")
+        u_pool8(1, 0, 1)
+        u_pool6(1, 0, 1)
+        finish_value(0, 0)
+        finish_value(0, 1)
+        v_pool(1, "X")
+        v_pool(1, "Y")
+        v_pool(1, "Z")
+        u_pool6(1, 1, 2)
+        u_pool8(1, 1, 2)
+        u_pool31(1)
+        scale_keys(1, 8)
+        scale_keys(1, 6)
+        store_keys(1)
+        finish_value(1, 0)
+        finish_value(1, 1)

@@ -309,19 +309,17 @@ def tile_afnb_pa_kernel(tc, low_feats, wk, bk, gk, bek, mk, vk, wv, bv, out_0, o
         def store_keys(b):
             nc.sync.dma_start(out=out_1[b].rearrange("(p k) l -> p k l", k=2), in_=state["ko", b][:])
 
-        nc.vector.memset(bvrow[:], 0.0)
         nc.vector.memset(warm[:], 1.0)
-        nc.vector.memset(ones[:], 1.0)
         nc.vector.memset(prm[:], 0.0)
-        load_wk(0)
-        nc.scalar.dma_start(out=bvrow[0:1, :], in_=bv.rearrange("(o c) -> o c", o=1))
-        load_wk(1)
+        nc.gpsimd.memset(bvrow[:], 0.0)
+        nc.sync.dma_start(out=w_u[:], in_=wk.rearrange("(p k) c -> p k c", k=2))
         load_wv(0)
         load_x(0, 0)
         load_wv(2)
         load_x(0, 1)
         for i, vec in enumerate((bk, gk, bek, mk, vk)):
             nc.sync.dma_start(out=prm[i : i + 1, :], in_=vec.rearrange("(o c) -> o c", o=1))
+        nc.sync.dma_start(out=bvrow[0:1, :], in_=bv.rearrange("(o c) -> o c", o=1))
         load_x(1, 0)
         load_x(1, 1)
         nc.scalar.activation(out=warm[:], in_=warm[:], func=ACT.Sqrt)
@@ -332,6 +330,7 @@ def tile_afnb_pa_kernel(tc, low_feats, wk, bk, gk, bek, mk, vk, wv, bv, out_0, o
         nc.gpsimd.memset(r4[:, 2:3], 16.0)
         nc.gpsimd.memset(r4[:, 3:4], 9.0)
         nc.gpsimd.memset(wloc[:], 1.0)
+        nc.gpsimd.memset(ones[:], 1.0)
         nc.gpsimd.memset(xg[:].rearrange("p (a c) -> p a c", a=4)[:, :, 4 * NPX : 4 * CW], 0.0)
         for qt, off, grid, bs in ((q8, 46, 8, 3), (q6, 10, 6, 4), (q3, 1, 3, 8)):
             nc.vector.tensor_copy(
@@ -368,14 +367,11 @@ def tile_afnb_pa_kernel(tc, low_feats, wk, bk, gk, bek, mk, vk, wv, bv, out_0, o
                 in1=q6[:, 3 * h : 3 * h + 3 : 2, :].unsqueeze(2).to_broadcast([P, 2, 2, 24]),
                 op=ALU.add,
             )
-        pbv = psum.tile([P, CV], F32, tag="T0", name="pbv")
-        nc.tensor.matmul(out=pbv[:], lhsT=ones[:], rhs=bvrow[:], start=True, stop=True)
         aux = psum.tile([P, 5, P], BF16, tag="T1", name="aux")
         for j in range(3):
             nc.tensor.transpose(
                 out=aux[:, j, :], in_=muni[:, P * j : P * j + P], identity=ident_b[:]
             )
-        nc.scalar.copy(out=bvb[:], in_=pbv[:])
         pu0 = weight_transposes(w_u[:, 0, :].bitcast(F32), "U0")
         pu1 = weight_transposes(w_u[:, 1, :].bitcast(F32), "U1")
         weight_copy(CV, pu0, False)
@@ -402,11 +398,14 @@ def tile_afnb_pa_kernel(tc, low_feats, wk, bk, gk, bek, mk, vk, wv, bv, out_0, o
         nc.vector.tensor_copy(out=prmt[:].rearrange("p v k -> p k v"), in_=aux[:, 3:5, 0:5])
         nc.vector.tensor_scalar_add(out=sc[:], in0=prmt[:, 4, :], scalar1=EPS)
         weight_quant(0, CV, (1,))
+        pbv = psum.tile([P, CV], F32, tag="T0", name="pbv")
+        nc.tensor.matmul(out=pbv[:], lhsT=ones[:], rhs=bvrow[:], start=True, stop=True)
         v_mx(0, "X", 0)
         v_mx(0, "Y", 0)
         v_mx(0, "Z", 0)
         regroup_vector(0, 1)
         regroup_scalar(0, 1)
+        nc.scalar.copy(out=bvb[:], in_=pbv[:])
         nc.scalar.activation(out=sc[:], in_=sc[:], func=ACT.Sqrt)
         quant_x(0, 1)
         nc.vector.reciprocal(out=sc[:], in_=sc[:])

@@ -44,6 +44,7 @@ def tile_afnb_pa_kernel(tc, low_feats, wk, bk, gk, bek, mk, vk, wv, bv, out_0, o
                 row.append(xr_bg)
             xr.append(row)
         ident_b = keep.tile([P, P], BF16)
+        busy_in = keep.tile([P, 256], F32)
         ident_f = keep.tile([P, P], F32)
         warm = keep.tile([P, 1], F32)
         q8 = keep.tile([P, 8, 24], BF16)
@@ -85,6 +86,11 @@ def tile_afnb_pa_kernel(tc, low_feats, wk, bk, gk, bek, mk, vk, wv, bv, out_0, o
             nc.sync.dma_start(
                 out=w_v[:, r0 : r0 + 2, :],
                 in_=wv[P * r0 : P * r0 + 256, :].rearrange("(r p) k -> p r k", p=P),
+            )
+
+        def keep_tensor_busy():
+            nc.tensor.matmul(
+                out=busy_out[:], lhsT=ident_f[:], rhs=busy_in[:], start=True, stop=True
             )
 
         def weight_transposes(words, bank):
@@ -310,13 +316,14 @@ def tile_afnb_pa_kernel(tc, low_feats, wk, bk, gk, bek, mk, vk, wv, bv, out_0, o
             nc.sync.dma_start(out=out_1[b].rearrange("(p k) l -> p k l", k=2), in_=state["ko", b][:])
 
         nc.vector.memset(warm[:], 1.0)
+        nc.vector.memset(busy_in[:], 1.0)
         nc.vector.memset(prm[:], 0.0)
         nc.gpsimd.memset(bvrow[:], 0.0)
+        load_x(0, 0)
         nc.sync.dma_start(out=w_u[:], in_=wk.rearrange("(p k) c -> p k c", k=2))
         load_wv(0)
-        load_x(0, 0)
-        load_wv(2)
         load_x(0, 1)
+        load_wv(2)
         for i, vec in enumerate((bk, gk, bek, mk, vk)):
             nc.sync.dma_start(out=prm[i : i + 1, :], in_=vec.rearrange("(o c) -> o c", o=1))
         nc.sync.dma_start(out=bvrow[0:1, :], in_=bv.rearrange("(o c) -> o c", o=1))
@@ -367,32 +374,41 @@ def tile_afnb_pa_kernel(tc, low_feats, wk, bk, gk, bek, mk, vk, wv, bv, out_0, o
                 in1=q6[:, 3 * h : 3 * h + 3 : 2, :].unsqueeze(2).to_broadcast([P, 2, 2, 24]),
                 op=ALU.add,
             )
+        busy_out = psum.tile([P, 256], F32, tag="T0", name="busy_out")
+        keep_tensor_busy()
+        keep_tensor_busy()
         aux = psum.tile([P, 5, P], BF16, tag="T1", name="aux")
         for j in range(3):
             nc.tensor.transpose(
                 out=aux[:, j, :], in_=muni[:, P * j : P * j + P], identity=ident_b[:]
             )
+        regroup_vector(0, 0)
+        regroup_scalar(0, 0)
+        keep_tensor_busy()
         pu0 = weight_transposes(w_u[:, 0, :].bitcast(F32), "U0")
         pu1 = weight_transposes(w_u[:, 1, :].bitcast(F32), "U1")
         weight_copy(CV, pu0, False)
+        quant_x(0, 0)
         weight_copy(CV + P, pu1, True)
+        keep_tensor_busy()
         pw0 = weight_transposes(w_v[:, 0, :].bitcast(F32), "X")
         pw1 = weight_transposes(w_v[:, 1, :].bitcast(F32), "Y")
         weight_copy(0, pw0, False)
-        weight_quant(CV, CH)
-        regroup_vector(0, 0)
-        regroup_scalar(0, 0)
         weight_copy(P, pw1, True)
-        quant_x(0, 0)
+        weight_quant(CV, CH)
+        regroup_vector(0, 1)
+        regroup_scalar(0, 1)
+        keep_tensor_busy()
         pw2 = weight_transposes(w_v[:, 2, :].bitcast(F32), "Z")
         pw3 = weight_transposes(w_v[:, 3, :].bitcast(F32), "U2")
-        weight_copy(2 * P, pw2, False)
-        weight_copy(3 * P, pw3, False)
-        weight_quant(0, CV, (0,))
         u_open(0)
         u_win(0, 0, 0, (0,))
         u_win(0, 1, 0, (0,))
         u_win(0, 0, 2, (0,))
+        weight_copy(2 * P, pw2, False)
+        quant_x(0, 1)
+        weight_copy(3 * P, pw3, False)
+        weight_quant(0, CV, (0,))
         for k in range(2):
             nc.tensor.transpose(out=aux[:, 3 + k, :], in_=prm[:, k:256:2], identity=ident_b[:])
         nc.vector.tensor_copy(out=prmt[:].rearrange("p v k -> p k v"), in_=aux[:, 3:5, 0:5])
@@ -400,69 +416,66 @@ def tile_afnb_pa_kernel(tc, low_feats, wk, bk, gk, bek, mk, vk, wv, bv, out_0, o
         weight_quant(0, CV, (1,))
         pbv = psum.tile([P, CV], F32, tag="T0", name="pbv")
         nc.tensor.matmul(out=pbv[:], lhsT=ones[:], rhs=bvrow[:], start=True, stop=True)
-        v_mx(0, "X", 0)
-        v_mx(0, "Y", 0)
-        v_mx(0, "Z", 0)
-        regroup_vector(0, 1)
-        regroup_scalar(0, 1)
-        nc.scalar.copy(out=bvb[:], in_=pbv[:])
-        nc.scalar.activation(out=sc[:], in_=sc[:], func=ACT.Sqrt)
-        quant_x(0, 1)
-        nc.vector.reciprocal(out=sc[:], in_=sc[:])
-        nc.gpsimd.tensor_tensor(out=bi[:], in0=prmt[:, 0, :], in1=prmt[:, 3, :], op=ALU.subtract)
-        nc.gpsimd.tensor_tensor(out=sc[:], in0=sc[:], in1=prmt[:, 1, :], op=ALU.mult)
-        nc.gpsimd.tensor_tensor(out=bi[:], in0=bi[:], in1=sc[:], op=ALU.mult)
-        nc.gpsimd.tensor_tensor(out=bi[:], in0=bi[:], in1=prmt[:, 2, :], op=ALU.add)
-        v_mx(0, "X", 1)
         u_win(0, 0, 0, (1,))
         u_win(0, 1, 0, (1,))
         u_win(0, 0, 2, (1,))
         u_win(0, 0, 1)
         u_win(0, 1, 1)
         u_win(0, 1, 2)
+        v_mx(0, "X", 0)
+        v_mx(0, "X", 1)
+        nc.scalar.copy(out=bvb[:], in_=pbv[:])
+        nc.scalar.activation(out=sc[:], in_=sc[:], func=ACT.Sqrt)
+        v_mx(0, "Y", 0)
         v_mx(0, "Y", 1)
+        v_mx(0, "Z", 0)
         v_mx(0, "Z", 1)
+        nc.vector.reciprocal(out=sc[:], in_=sc[:])
+        nc.gpsimd.tensor_tensor(out=bi[:], in0=prmt[:, 0, :], in1=prmt[:, 3, :], op=ALU.subtract)
+        nc.gpsimd.tensor_tensor(out=sc[:], in0=sc[:], in1=prmt[:, 1, :], op=ALU.mult)
+        nc.gpsimd.tensor_tensor(out=bi[:], in0=bi[:], in1=sc[:], op=ALU.mult)
+        nc.gpsimd.tensor_tensor(out=bi[:], in0=bi[:], in1=prmt[:, 2, :], op=ALU.add)
         regroup_vector(1, 0)
         regroup_scalar(1, 0)
-        quant_x(1, 0)
-        v_copy(0, "X", False)
-        u_relu(0, 0)
-        regroup_vector(1, 1)
-        regroup_scalar(1, 1)
         nc.vector.tensor_tensor(
             out=pmat[:], in0=aux[:, 0:3, :], in1=wloc[:].unsqueeze(1).to_broadcast([P, 3, P]), op=ALU.mult
         )
-        quant_x(1, 1)
-        v_copy(0, "Y", False)
-        v_copy(0, "Z", False)
+        u_relu(0, 0)
+        quant_x(1, 0)
+        v_copy(0, "X", False)
+        regroup_vector(1, 1)
+        regroup_scalar(1, 1)
         u_relu(0, 1)
+        v_copy(0, "Y", True)
+        quant_x(1, 1)
+        v_copy(0, "Z", False)
         v_pool(0, "X")
+        v_pool(0, "Y")
+        v_pool(0, "Z")
         v_mx(1, "X", 0)
         v_mx(1, "Y", 0)
         v_mx(1, "Z", 0)
-        v_mx(1, "X", 1)
-        v_copy(1, "X", False)
-        v_mx(1, "Y", 1)
-        v_copy(1, "Y", False)
-        u_pool8(0, 0, 2)
-        u_pool6(0, 0, 2)
-        u_pool31(0)
-        scale_keys(0, 8)
-        scale_keys(0, 6)
-        store_keys(0)
         u_open(1)
         u_mx(1, 0)
         u_relu(1, 0)
         u_mx(1, 1)
         u_relu(1, 1)
+        u_pool8(0, 0, 2)
+        v_mx(1, "X", 1)
+        v_copy(1, "X", False)
+        v_mx(1, "Y", 1)
+        v_copy(1, "Y", False)
         v_mx(1, "Z", 1)
         v_copy(1, "Z", False)
-        v_pool(0, "Y")
-        v_pool(0, "Z")
-        u_pool8(1, 0, 1)
-        u_pool6(1, 0, 1)
+        u_pool6(0, 0, 2)
+        u_pool31(0)
+        scale_keys(0, 8)
+        scale_keys(0, 6)
+        store_keys(0)
         finish_value(0, 0)
         finish_value(0, 1)
+        u_pool8(1, 0, 1)
+        u_pool6(1, 0, 1)
         v_pool(1, "X")
         v_pool(1, "Y")
         v_pool(1, "Z")

@@ -61,6 +61,7 @@ def tile_afnb_pa_kernel(tc, low_feats, wk, bk, gk, bek, mk, vk, wv, bv, out_0, o
         sums3 = keep.tile([P, NB, 2, 9], F32)
         sums1 = keep.tile([P, NB, 2], F32)
         prmt = keep.tile([P, 5, 2], F32)
+        eps = keep.tile([P, 1], F32)
         sc = keep.tile([P, 2], F32)
         bi = keep.tile([P, 2], F32)
         wg = keep.tile([P, 2 * CH * 4], BF16, align_bytes=64)
@@ -170,15 +171,18 @@ def tile_afnb_pa_kernel(tc, low_feats, wk, bk, gk, bek, mk, vk, wv, bv, out_0, o
         def u_open(b):
             for k in range(2):
                 state["pu", b, k] = psum.tile([P, 384], F32, tag="U%d" % k, name="pu%d_%d" % (k, b))
+
+        def u_open_tail(b):
             state["pu", b, 2] = psum.tile([P, 2, 256], F32, tag="U2", name="pu2_%d" % b)
 
         def u_win(b, k, win, gs=(0, 1)):
             w0 = CV + P * k
-            out, lo, n = (
-                (state["pu", b, k][:, 0:256], 0, 256),
-                (state["pu", b, k][:, 256:384], 256, 128),
-                (state["pu", b, 2][:, k, :], 384, 256),
-            )[win]
+            if win < 2:
+                lo, n = ((0, 256), (256, 128))[win]
+                out = state["pu", b, k][:, lo : lo + n]
+            else:
+                lo, n = 384, 256
+                out = state["pu", b, 2][:, k, :]
             for g in gs:
                 x0 = xcol(b, g) + lo
                 nc.tensor.matmul_mx(
@@ -323,10 +327,10 @@ def tile_afnb_pa_kernel(tc, low_feats, wk, bk, gk, bek, mk, vk, wv, bv, out_0, o
         nc.sync.dma_start(out=w_u[:], in_=wk.rearrange("(p k) c -> p k c", k=2))
         load_wv(0)
         load_x(0, 1)
+        nc.sync.dma_start(out=bvrow[0:1, :], in_=bv.rearrange("(o c) -> o c", o=1))
         load_wv(2)
         for i, vec in enumerate((bk, gk, bek, mk, vk)):
             nc.sync.dma_start(out=prm[i : i + 1, :], in_=vec.rearrange("(o c) -> o c", o=1))
-        nc.sync.dma_start(out=bvrow[0:1, :], in_=bv.rearrange("(o c) -> o c", o=1))
         load_x(1, 0)
         load_x(1, 1)
         nc.scalar.activation(out=warm[:], in_=warm[:], func=ACT.Sqrt)
@@ -338,6 +342,7 @@ def tile_afnb_pa_kernel(tc, low_feats, wk, bk, gk, bek, mk, vk, wv, bv, out_0, o
         nc.gpsimd.memset(r4[:, 3:4], 9.0)
         nc.gpsimd.memset(wloc[:], 1.0)
         nc.gpsimd.memset(ones[:], 1.0)
+        nc.gpsimd.memset(eps[:], EPS)
         nc.gpsimd.memset(xg[:].rearrange("p (a c) -> p a c", a=4)[:, :, 4 * NPX : 4 * CW], 0.0)
         for qt, off, grid, bs in ((q8, 46, 8, 3), (q6, 10, 6, 4), (q3, 1, 3, 8)):
             nc.vector.tensor_copy(
@@ -374,14 +379,17 @@ def tile_afnb_pa_kernel(tc, low_feats, wk, bk, gk, bek, mk, vk, wv, bv, out_0, o
                 in1=q6[:, 3 * h : 3 * h + 3 : 2, :].unsqueeze(2).to_broadcast([P, 2, 2, 24]),
                 op=ALU.add,
             )
-        busy_out = psum.tile([P, 256], F32, tag="T0", name="busy_out")
-        keep_tensor_busy()
+        busy_out = psum.tile([P, 256], F32, tag="Z", name="busy_out")
         keep_tensor_busy()
         aux = psum.tile([P, 5, P], BF16, tag="T1", name="aux")
         for j in range(3):
             nc.tensor.transpose(
                 out=aux[:, j, :], in_=muni[:, P * j : P * j + P], identity=ident_b[:]
             )
+        nc.vector.tensor_tensor(
+            out=pmat[:], in0=aux[:, 0:3, :], in1=wloc[:].unsqueeze(1).to_broadcast([P, 3, P]), op=ALU.mult
+        )
+        keep_tensor_busy()
         regroup_vector(0, 0)
         regroup_scalar(0, 0)
         keep_tensor_busy()
@@ -393,80 +401,75 @@ def tile_afnb_pa_kernel(tc, low_feats, wk, bk, gk, bek, mk, vk, wv, bv, out_0, o
         keep_tensor_busy()
         pw0 = weight_transposes(w_v[:, 0, :].bitcast(F32), "X")
         pw1 = weight_transposes(w_v[:, 1, :].bitcast(F32), "Y")
-        weight_copy(0, pw0, False)
-        weight_copy(P, pw1, True)
+        regroup_scalar(0, 1)
         weight_quant(CV, CH)
         regroup_vector(0, 1)
-        regroup_scalar(0, 1)
-        keep_tensor_busy()
-        pw2 = weight_transposes(w_v[:, 2, :].bitcast(F32), "Z")
-        pw3 = weight_transposes(w_v[:, 3, :].bitcast(F32), "U2")
+        weight_copy(P, pw1, True)
         u_open(0)
         u_win(0, 0, 0, (0,))
         u_win(0, 1, 0, (0,))
-        u_win(0, 0, 2, (0,))
-        weight_copy(2 * P, pw2, False)
+        weight_copy(0, pw0, False)
         quant_x(0, 1)
-        weight_copy(3 * P, pw3, False)
-        weight_quant(0, CV, (0,))
-        for k in range(2):
-            nc.tensor.transpose(out=aux[:, 3 + k, :], in_=prm[:, k:256:2], identity=ident_b[:])
-        nc.vector.tensor_copy(out=prmt[:].rearrange("p v k -> p k v"), in_=aux[:, 3:5, 0:5])
-        nc.vector.tensor_scalar_add(out=sc[:], in0=prmt[:, 4, :], scalar1=EPS)
-        weight_quant(0, CV, (1,))
         pbv = psum.tile([P, CV], F32, tag="T0", name="pbv")
         nc.tensor.matmul(out=pbv[:], lhsT=ones[:], rhs=bvrow[:], start=True, stop=True)
+        pw2 = weight_transposes(w_v[:, 2, :].bitcast(F32), "Z")
+        pw3 = weight_transposes(w_v[:, 3, :].bitcast(F32), "U2")
+        weight_copy(2 * P, pw2, False)
+        weight_copy(3 * P, pw3, True)
+        for k in range(2):
+            nc.tensor.transpose(out=aux[:, 3 + k, :], in_=prm[:, k:256:2], identity=ident_b[:])
+        u_open_tail(0)
         u_win(0, 0, 0, (1,))
         u_win(0, 1, 0, (1,))
-        u_win(0, 0, 2, (1,))
         u_win(0, 0, 1)
+        u_win(0, 0, 2)
         u_win(0, 1, 1)
         u_win(0, 1, 2)
-        v_mx(0, "X", 0)
-        v_mx(0, "X", 1)
+        nc.scalar.copy(out=prmt[:].rearrange("p v k -> p k v"), in_=aux[:, 3:5, 0:5])
+        nc.scalar.activation(out=sc[:], in_=prmt[:, 4, :], func=ACT.Sqrt, bias=eps[:, 0:1])
+        weight_quant(0, CV)
         nc.scalar.copy(out=bvb[:], in_=pbv[:])
-        nc.scalar.activation(out=sc[:], in_=sc[:], func=ACT.Sqrt)
-        v_mx(0, "Y", 0)
-        v_mx(0, "Y", 1)
-        v_mx(0, "Z", 0)
-        v_mx(0, "Z", 1)
         nc.vector.reciprocal(out=sc[:], in_=sc[:])
         nc.gpsimd.tensor_tensor(out=bi[:], in0=prmt[:, 0, :], in1=prmt[:, 3, :], op=ALU.subtract)
         nc.gpsimd.tensor_tensor(out=sc[:], in0=sc[:], in1=prmt[:, 1, :], op=ALU.mult)
         nc.gpsimd.tensor_tensor(out=bi[:], in0=bi[:], in1=sc[:], op=ALU.mult)
         nc.gpsimd.tensor_tensor(out=bi[:], in0=bi[:], in1=prmt[:, 2, :], op=ALU.add)
+        v_mx(0, "X", 0)
+        v_mx(0, "X", 1)
+        v_mx(0, "Y", 0)
+        v_mx(0, "Y", 1)
+        v_mx(0, "Z", 0)
+        v_mx(0, "Z", 1)
         regroup_vector(1, 0)
         regroup_scalar(1, 0)
-        nc.vector.tensor_tensor(
-            out=pmat[:], in0=aux[:, 0:3, :], in1=wloc[:].unsqueeze(1).to_broadcast([P, 3, P]), op=ALU.mult
-        )
-        u_relu(0, 0)
-        quant_x(1, 0)
         v_copy(0, "X", False)
+        quant_x(1, 0)
+        u_relu(0, 0)
         regroup_vector(1, 1)
         regroup_scalar(1, 1)
-        u_relu(0, 1)
         v_copy(0, "Y", True)
         quant_x(1, 1)
         v_copy(0, "Z", False)
+        u_relu(0, 1)
         v_pool(0, "X")
         v_pool(0, "Y")
-        v_pool(0, "Z")
+        u_open(1)
+        u_open_tail(1)
         v_mx(1, "X", 0)
         v_mx(1, "Y", 0)
-        v_mx(1, "Z", 0)
-        u_open(1)
+        v_pool(0, "Z")
         u_mx(1, 0)
         u_relu(1, 0)
         u_mx(1, 1)
         u_relu(1, 1)
-        u_pool8(0, 0, 2)
+        v_mx(1, "Z", 0)
         v_mx(1, "X", 1)
         v_copy(1, "X", False)
         v_mx(1, "Y", 1)
         v_copy(1, "Y", False)
         v_mx(1, "Z", 1)
         v_copy(1, "Z", False)
+        u_pool8(0, 0, 2)
         u_pool6(0, 0, 2)
         u_pool31(0)
         scale_keys(0, 8)

@@ -17,7 +17,6 @@ NB = 2
 NPX = 576
 CW = 640
 CV = 512
-CH = 768
 NLOC = 110
 EPS = 1e-5
 FLOPS = 2 * 768 * 1024 * 1152
@@ -54,20 +53,29 @@ def tile_afnb_pa_kernel(tc, low_feats, wk, bk, gk, bek, mk, vk, wv, bv, out_0, o
         pmat = keep.tile([P, 3, P], F32)
         wloc = keep.tile([P, P], F32)
         r4 = keep.tile([P, 4], F32)
-        bvb = keep.tile([P, CV], F32)
+        bvb = keep.tile([P, 256], F32)
+        sv = keep.tile([P, NB, 2, P], F32)
+        hsum = keep.tile([P, NB, 2, 96], F32)
+        s0p = keep.tile([P, NB, 2, 24], F32)
+        vhalf = keep.tile([P, NB, 2, 18], F32)
+        rs = keep.tile([P, 1], F32)
+        rtmp = keep.tile([P, NLOC], F32)
         sums8 = keep.tile([P, NB, 2, 64], F32)
         sums6 = keep.tile([P, NB, 2, 36], F32)
-        half = keep.tile([P, NB, 2, 18], F32)
-        sums3 = keep.tile([P, NB, 2, 9], F32)
-        sums1 = keep.tile([P, NB, 2], F32)
+        half = keep.tile([P, 2 * NB, 18], F32)
+        sums3 = keep.tile([P, 2 * NB, 9], F32)
+        sums1 = keep.tile([P, 2 * NB], F32)
+        ko = keep.tile([P, NB, 2, NLOC], F32)
         prmt = keep.tile([P, 5, 2], F32)
         eps = keep.tile([P, 1], F32)
         sc = keep.tile([P, 2], F32)
         bi = keep.tile([P, 2], F32)
-        wg = keep.tile([P, 2 * CH * 4], BF16, align_bytes=64)
-        wgf = wg[:].bitcast(F32).rearrange("p (g c u) -> p g c u", g=2, u=2)
-        wc = keep.tile([P, 2 * CH], U32, align_bytes=64)
-        wsc = keep.tile([P, 2 * CH], U8, align_bytes=64)
+        wg, wc, wsc = {}, {}, {}
+        for grp in "uab":
+            wg_t = keep.tile([P, 2048], BF16, align_bytes=64, name="wg_" + grp)
+            wc_t = keep.tile([P, 512], U32, align_bytes=64, name="wc_" + grp)
+            ws_t = keep.tile([P, 512], U8, align_bytes=64, name="ws_" + grp)
+            wg[grp], wc[grp], wsc[grp] = wg_t, wc_t, ws_t
         xg = keep.tile([P, 4 * CW * 4], BF16, align_bytes=64)
         xc = keep.tile([P, 4 * CW], U32, align_bytes=64)
         xs = keep.tile([P, 4 * CW], U8, align_bytes=64)
@@ -105,22 +113,24 @@ def tile_afnb_pa_kernel(tc, low_feats, wk, bk, gk, bek, mk, vk, wv, bv, out_0, o
                     )
             return pw
 
-        def weight_copy(c0, pw, on_vector):
-            dst = wgf[:, :, c0 : c0 + P, :]
+        def weight_copy(grp, k, pw, on_vector):
+            words = wg[grp][:].bitcast(F32)
+            if grp == "a":
+                dst = words.rearrange("p (g k c u) -> p g k c u", g=2, k=2, u=2)[:, :, k, :, :]
+            else:
+                dst = words.rearrange("p (k g c u) -> p k g c u", k=2, g=2, u=2)[:, k, :, :, :]
             src = pw[:].rearrange("p g u c -> p g c u")
             if on_vector:
                 nc.vector.tensor_copy(out=dst, in_=src)
             else:
                 nc.scalar.copy(out=dst, in_=src)
 
-        def weight_quant(c0, c1, gs=(0, 1)):
-            for g in gs:
-                lo = g * CH + c0
-                hi = g * CH + c1
+        def weight_quant(grp, parts=((0, 256), (256, 512))):
+            for lo, hi in parts:
                 nc.vector.quantize_mx(
-                    out=wc[:, lo:hi].bitcast(FP8X4),
-                    scales=wsc[:, lo:hi],
-                    in_=wg[:, 4 * lo : 4 * hi],
+                    out=wc[grp][:, lo:hi].bitcast(FP8X4),
+                    scales=wsc[grp][:, lo:hi],
+                    in_=wg[grp][:, 4 * lo : 4 * hi],
                 )
 
         def xcol(b, g):
@@ -176,7 +186,6 @@ def tile_afnb_pa_kernel(tc, low_feats, wk, bk, gk, bek, mk, vk, wv, bv, out_0, o
             state["pu", b, 2] = psum.tile([P, 2, 256], F32, tag="U2", name="pu2_%d" % b)
 
         def u_win(b, k, win, gs=(0, 1)):
-            w0 = CV + P * k
             if win < 2:
                 lo, n = ((0, 256), (256, 128))[win]
                 out = state["pu", b, k][:, lo : lo + n]
@@ -185,10 +194,11 @@ def tile_afnb_pa_kernel(tc, low_feats, wk, bk, gk, bek, mk, vk, wv, bv, out_0, o
                 out = state["pu", b, 2][:, k, :]
             for g in gs:
                 x0 = xcol(b, g) + lo
+                w0 = P * (2 * k + g)
                 nc.tensor.matmul_mx(
                     out=out,
-                    lhsT=wc[:, g * CH + w0 : g * CH + w0 + P].bitcast(FP8X4),
-                    lhsT_scale=wsc[:, g * CH + w0 : g * CH + w0 + P],
+                    lhsT=wc["u"][:, w0 : w0 + P].bitcast(FP8X4),
+                    lhsT_scale=wsc["u"][:, w0 : w0 + P],
                     rhs=xc[:, x0 : x0 + n].bitcast(FP8X4),
                     rhs_scale=xs[:, x0 : x0 + n],
                     start=(g == 0),
@@ -223,48 +233,155 @@ def tile_afnb_pa_kernel(tc, low_feats, wk, bk, gk, bek, mk, vk, wv, bv, out_0, o
                     out=dst, in_=src, func=ACT.Relu, bias=bi[:, k : k + 1], scale=sc[:, k : k + 1]
                 )
 
-        V_PASSES = {"X": (0, 384), "Y": (128, 512), "Z": (256,)}
+        PX_PASSES = {"X": (0, 384), "Y": (128, 512), "Z": (256,)}
 
-        def v_mx(b, bank, g):
-            if g == 0:
-                state[bank, b] = psum.tile([P, CV], F32, tag=bank, name="pv%s%d" % (bank, b))
-            offs = V_PASSES[bank]
-            for i, off in enumerate(offs):
-                x0 = xcol(b, g) + off
-                nc.tensor.matmul_mx(
-                    out=state[bank, b][:],
-                    lhsT=xc[:, x0 : x0 + P].bitcast(FP8X4),
-                    lhsT_scale=xs[:, x0 : x0 + P],
-                    rhs=wc[:, g * CH : g * CH + CV].bitcast(FP8X4),
-                    rhs_scale=wsc[:, g * CH : g * CH + CV],
-                    start=(g == 0 and i == 0),
-                    stop=(g == 1 and i == len(offs) - 1),
-                )
+        def px_mx(b, part, gs=(0, 1)):
+            if 0 in gs:
+                if part == "X":
+                    state["X", b] = psum.tile([P, 256], F32, tag="A", name="pxa%d" % b)
+                elif part == "Y":
+                    yz = psum.tile([P, 2, 256], F32, tag="B", name="pxb%d" % b)
+                    state["Y", b] = yz[:, 0, :]
+                    state["Z", b] = yz[:, 1, :]
+            out = state[part, b]
+            offs = PX_PASSES[part]
+            for g in gs:
+                for i, off in enumerate(offs):
+                    x0 = xcol(b, g) + off
+                    nc.tensor.matmul_mx(
+                        out=out[:] if part == "X" else out,
+                        lhsT=xc[:, x0 : x0 + P].bitcast(FP8X4),
+                        lhsT_scale=xs[:, x0 : x0 + P],
+                        rhs=wc["a"][:, 256 * g : 256 * g + 256].bitcast(FP8X4),
+                        rhs_scale=wsc["a"][:, 256 * g : 256 * g + 256],
+                        start=(g == 0 and i == 0),
+                        stop=(g == 1 and i == len(offs) - 1),
+                    )
 
-        def v_copy(b, bank, on_vector):
-            vsb = work.tile([P, CV], F32, tag="v" + bank, name="vsb%s%d" % (bank, b))
-            state["v" + bank, b] = vsb
+        def px_copy(b, part, on_vector):
+            vsb = work.tile([P, 256], F32, tag="v" + part, name="vsb%s%d" % (part, b))
+            state["v" + part, b] = vsb
+            src = state[part, b][:] if part == "X" else state[part, b]
             if on_vector:
-                nc.vector.tensor_copy(out=vsb[:], in_=state[bank, b][:])
+                nc.vector.tensor_copy(out=vsb[:], in_=src)
             else:
-                nc.scalar.copy(out=vsb[:], in_=state[bank, b][:])
+                nc.scalar.copy(out=vsb[:], in_=src)
 
-        def v_pool(b, bank):
+        def px_copy_yz(b):
+            vsb = work.tile([P, 2, 256], F32, tag="vYZ", name="vsbyz%d" % b)
+            nc.scalar.copy(out=vsb[:, 0, :], in_=state["Y", b])
+            nc.scalar.copy(out=vsb[:, 1, :], in_=state["Z", b])
+            state["vY", b] = vsb[:, 0, :]
+            state["vZ", b] = vsb[:, 1, :]
+
+        def px_bias(b):
+            state["pt", b] = psum.tile([P, CV], F32, tag="T", name="pt%d" % b)
+            nc.tensor.matmul(
+                out=state["pt", b][:, 0:256], lhsT=ones[:], rhs=bvrow[:, 0:256], start=True, stop=False
+            )
+
+        def px_pool(b, part):
+            nc.tensor.matmul(
+                out=state["pt", b][:, 0:256], lhsT=pmat[:, "XYZ".index(part), :],
+                rhs=state["v" + part, b][:], start=False, stop=(part == "Z"),
+            )
+
+        def cm_mx(b, k):
+            pc = psum.tile([P, 384], F32, tag="C%d" % k, name="pc%d%d" % (b, k))
+            state["pc", b, k] = pc
+            for lo, n, offs in ((0, 256, (0, 384)), (256, 128, (256,))):
+                for g in range(2):
+                    w0 = P * (2 * k + g)
+                    for i, off in enumerate(offs):
+                        x0 = xcol(b, g) + off
+                        nc.tensor.matmul_mx(
+                            out=pc[:, lo : lo + n],
+                            lhsT=wc["b"][:, w0 : w0 + P].bitcast(FP8X4),
+                            lhsT_scale=wsc["b"][:, w0 : w0 + P],
+                            rhs=xc[:, x0 : x0 + n].bitcast(FP8X4),
+                            rhs_scale=xs[:, x0 : x0 + n],
+                            start=(g == 0 and i == 0),
+                            stop=(g == 1 and i == len(offs) - 1),
+                        )
+
+        def cm_pool(b, k):
+            pc = state["pc", b, k]
+            nc.vector.tensor_reduce(
+                out=sv[:, b, k, 46:110], in_=pc[:].rearrange("p (t a j) -> p a t j", t=2, j=3),
+                axis=AX.XY, op=ALU.add,
+            )
+            nc.vector.tensor_reduce(
+                out=hsum[:, b, k, :], in_=pc[:].rearrange("p (a j) -> p a j", j=4),
+                axis=AX.X, op=ALU.add,
+            )
+
+        def cm_rows(b):
+            add = ALU.add
+            rows = hsum[:, b, :, :].rearrange("p k (r c) -> p k r c", c=6)
+            six = sv[:, b, :, 10:46].rearrange("p k (r c) -> p k r c", c=6)
+            pair = s0p[:, b, :, :].rearrange("p k (a c) -> p k a c", c=6)
+            nc.gpsimd.tensor_tensor(
+                out=pair, in0=rows[:, :, 8:16:2, :], in1=rows[:, :, 9:16:2, :], op=add
+            )
+            nc.gpsimd.tensor_tensor(
+                out=six[:, :, 1:6:3, :], in0=rows[:, :, 1:8:4, :], in1=rows[:, :, 2:8:4, :], op=add
+            )
             for h in range(2):
-                if bank == "X":
-                    state["pt", b, h] = psum.tile([P, 256], F32, tag="T%d" % h, name="pt%d%d" % (b, h))
-                nc.tensor.matmul(
-                    out=state["pt", b, h][:], lhsT=pmat[:, "XYZ".index(bank), :],
-                    rhs=state["v" + bank, b][:, 256 * h : 256 * h + 256],
-                    start=(bank == "X"), stop=(bank == "Z"),
+                nc.gpsimd.tensor_tensor(
+                    out=six[:, :, 3 * h : 3 * h + 3 : 2, :], in0=rows[:, :, 4 * h : 4 * h + 4 : 3, :],
+                    in1=pair[:, :, 2 * h : 2 * h + 2, :], op=add,
+                )
+            halves = vhalf[:, b, :, :].rearrange("p k (m c) -> p k m c", c=3)
+            nc.gpsimd.tensor_tensor(
+                out=vhalf[:, b, :, :], in0=sv[:, b, :, 10:46:2], in1=sv[:, b, :, 11:46:2], op=add
+            )
+            nc.gpsimd.tensor_tensor(
+                out=sv[:, b, :, 1:10].rearrange("p k (g c) -> p k g c", c=3),
+                in0=halves[:, :, 0:6:2, :], in1=halves[:, :, 1:6:2, :], op=add,
+            )
+
+        def cm_total(b):
+            nc.vector.tensor_reduce(
+                out=sv[:, b, :, 0:1], in_=sv[:, b, :, 1:10], axis=AX.X, op=ALU.add
+            )
+
+        def cm_transposes(b):
+            for k in range(2):
+                nc.tensor.transpose(
+                    out=state["pt", b][:, 256 + P * k : 384 + P * k], in_=sv[:, b, k, :],
+                    identity=ident_f[:],
                 )
 
-        def finish_value(b, h):
-            vo = work.tile([P, 256], F32, tag="vo%d" % h, name="vo%d%d" % (b, h))
-            nc.vector.tensor_tensor(
-                out=vo[:], in0=state["pt", b, h][:], in1=bvb[:, 256 * h : 256 * h + 256], op=ALU.add
+        def finish_px(b):
+            vo = work.tile([P, 256], F32, tag="vo0", name="vo0%d" % b)
+            nc.scalar.copy(out=vo[:], in_=state["pt", b][:, 0:256])
+            nc.sync.dma_start(out=out_0[b, :, 0:256], in_=vo[0:NLOC, :])
+
+        def finish_cm(b):
+            vo = work.tile([P, 256], F32, tag="vo1", name="vo1%d" % b)
+            nc.vector.scalar_tensor_tensor(
+                out=vo[:], in0=state["pt", b][:, 256:512], scalar=rs[:, 0:1],
+                in1=bvb[:], op0=ALU.mult, op1=ALU.add,
             )
-            nc.sync.dma_start(out=out_0[b, :, 256 * h : 256 * h + 256], in_=vo[0:NLOC, :])
+            nc.sync.dma_start(out=out_0[b, :, 256:512], in_=vo[0:NLOC, :])
+
+        def u_pool6_gpsimd(b, k):
+            r_k = state["r", b][:, k, :]
+            tg = "%d%d" % (b, k)
+            rv2 = r_k.rearrange("p (m j) -> p m j", j=2)
+            p6 = work.tile([P, 288], F32, tag="p6", name="p6_" + tg)
+            nc.gpsimd.tensor_tensor(out=p6[:], in0=rv2[:, :, 0], in1=rv2[:, :, 1], op=ALU.add)
+            p6v = p6[:].rearrange("p (m j) -> p m j", j=2)
+            p6b = work.tile([P, 144], F32, tag="p6b", name="p6b_" + tg)
+            nc.gpsimd.tensor_tensor(out=p6b[:], in0=p6v[:, :, 0], in1=p6v[:, :, 1], op=ALU.add)
+            p6bv = p6b[:].rearrange("p (a e c) -> p a e c", e=2, c=6)
+            h6 = work.tile([P, 12, 6], F32, tag="h6", name="h6_" + tg)
+            nc.gpsimd.tensor_tensor(out=h6[:], in0=p6bv[:, :, 0, :], in1=p6bv[:, :, 1, :], op=ALU.add)
+            h6v = h6[:].rearrange("p (g a) c -> p g a c", a=2)
+            nc.gpsimd.tensor_tensor(
+                out=sums6[:, b, k, :].rearrange("p (g c) -> p g c", c=6),
+                in0=h6v[:, :, 0, :], in1=h6v[:, :, 1, :], op=ALU.add,
+            )
 
         def u_pool8(b, k0, k1):
             nc.vector.tensor_reduce(
@@ -284,63 +401,46 @@ def tile_afnb_pa_kernel(tc, low_feats, wk, bk, gk, bek, mk, vk, wv, bv, out_0, o
                 axis=AX.XY, op=ALU.add,
             )
 
-        def u_pool31(b):
+        def u_pool31():
+            six = sums6[:].rearrange("p b k l -> p (b k) l")
             nc.vector.tensor_reduce(
-                out=half[:, b, :, :],
-                in_=sums6[:, b, :, :].rearrange("p k (m j) -> p k m j", j=2),
-                axis=AX.X, op=ALU.add,
+                out=half[:], in_=six.rearrange("p a (m j) -> p a m j", j=2), axis=AX.X, op=ALU.add
             )
+            nc.vector.tensor_reduce(out=sums1[:], in_=six, axis=AX.X, op=ALU.add)
             nc.vector.tensor_reduce(
-                out=sums1[:, b, :], in_=sums6[:, b, :, :], axis=AX.X, op=ALU.add
-            )
-            nc.vector.tensor_reduce(
-                out=sums3[:, b, :, :].rearrange("p k (g c) -> p (k g) c", c=3),
-                in_=half[:, b, :, :].rearrange("p k (g i c) -> p (k g) c i", i=2, c=3),
+                out=sums3[:].rearrange("p a (g c) -> p (a g) c", c=3),
+                in_=half[:].rearrange("p a (g i c) -> p (a g) c i", i=2, c=3),
                 axis=AX.X, op=ALU.add,
             )
 
-        def scale_keys(b, which):
-            if which == 8:
-                state["ko", b] = work.tile([P, 2, NLOC], F32, tag="ko", name="ko%d" % b)
-            ko = state["ko", b]
-            for dst, src, count in (
-                ((ko[:, :, 46:110], sums8[:, b, :, :], 9),)
-                if which == 8
-                else (
-                    (ko[:, :, 10:46], sums6[:, b, :, :], 16),
-                    (ko[:, :, 1:10], sums3[:, b, :, :], 64),
-                    (ko[:, :, 0], sums1[:, b, :], 576),
-                )
-            ):
-                nc.gpsimd.tensor_scalar(
-                    out=dst, in0=src, scalar1=1.0 / count, scalar2=0.0, op0=ALU.mult, op1=ALU.add
-                )
+        kov = ko[:].rearrange("p b k l -> p (b k) l")
+
+        def scale_keys(dst, src, count):
+            nc.scalar.activation(out=dst, in_=src, func=ACT.Copy, scale=1.0 / count)
 
         def store_keys(b):
-            nc.sync.dma_start(out=out_1[b].rearrange("(p k) l -> p k l", k=2), in_=state["ko", b][:])
+            nc.sync.dma_start(out=out_1[b].rearrange("(p k) l -> p k l", k=2), in_=ko[:, b, :, :])
 
+        nc.vector.memset(bvrow[:], 0.0)
         nc.vector.memset(warm[:], 1.0)
-        nc.vector.memset(busy_in[:], 1.0)
         nc.vector.memset(prm[:], 0.0)
-        nc.gpsimd.memset(bvrow[:], 0.0)
+        nc.vector.memset(busy_in[:], 1.0)
+        nc.vector.memset(sv[:, :, :, NLOC:P], 0.0)
         load_x(0, 0)
         nc.sync.dma_start(out=w_u[:], in_=wk.rearrange("(p k) c -> p k c", k=2))
         load_wv(0)
-        load_x(0, 1)
         nc.sync.dma_start(out=bvrow[0:1, :], in_=bv.rearrange("(o c) -> o c", o=1))
+        load_x(0, 1)
         load_wv(2)
+        load_x(1, 0)
         for i, vec in enumerate((bk, gk, bek, mk, vk)):
             nc.sync.dma_start(out=prm[i : i + 1, :], in_=vec.rearrange("(o c) -> o c", o=1))
-        load_x(1, 0)
         load_x(1, 1)
         nc.scalar.activation(out=warm[:], in_=warm[:], func=ACT.Sqrt)
+        for i, count in enumerate((576.0, 64.0, 16.0, 9.0)):
+            nc.gpsimd.memset(r4[:, i : i + 1], count)
         make_identity(nc, ident_b[:])
         make_identity(nc, ident_f[:])
-        nc.gpsimd.memset(r4[:, 0:1], 576.0)
-        nc.gpsimd.memset(r4[:, 1:2], 64.0)
-        nc.gpsimd.memset(r4[:, 2:3], 16.0)
-        nc.gpsimd.memset(r4[:, 3:4], 9.0)
-        nc.gpsimd.memset(wloc[:], 1.0)
         nc.gpsimd.memset(ones[:], 1.0)
         nc.gpsimd.memset(eps[:], EPS)
         nc.gpsimd.memset(xg[:].rearrange("p (a c) -> p a c", a=4)[:, :, 4 * NPX : 4 * CW], 0.0)
@@ -353,11 +453,6 @@ def tile_afnb_pa_kernel(tc, low_feats, wk, bk, gk, bek, mk, vk, wv, bv, out_0, o
                 .to_broadcast([P, grid, grid, bs]),
             )
         nc.vector.reciprocal(out=r4[:], in_=r4[:])
-        for i, (lo, hi) in enumerate(((0, 1), (1, 10), (10, 46), (46, P))):
-            nc.gpsimd.tensor_scalar(
-                out=wloc[:, lo:hi], in0=wloc[:, lo:hi], scalar1=r4[:, i : i + 1], scalar2=0.0,
-                op0=ALU.mult, op1=ALU.add,
-            )
         q6r = q6[:].rearrange("p (g i) w -> p g i w", i=2)
         nc.vector.tensor_scalar_add(out=q3[:], in0=q3[:], scalar1=ident_f[:, 0:1])
         nc.vector.tensor_tensor(
@@ -379,9 +474,13 @@ def tile_afnb_pa_kernel(tc, low_feats, wk, bk, gk, bek, mk, vk, wv, bv, out_0, o
                 in1=q6[:, 3 * h : 3 * h + 3 : 2, :].unsqueeze(2).to_broadcast([P, 2, 2, 24]),
                 op=ALU.add,
             )
-        busy_out = psum.tile([P, 256], F32, tag="Z", name="busy_out")
+        for i, (lo, hi) in enumerate(((0, 1), (1, 10), (10, 46), (46, P))):
+            nc.vector.tensor_copy(
+                out=wloc[:, lo:hi], in_=r4[:, i : i + 1].to_broadcast([P, hi - lo])
+            )
+        busy_out = psum.tile([P, 256], F32, tag="C0", name="busy_out")
         keep_tensor_busy()
-        aux = psum.tile([P, 5, P], BF16, tag="T1", name="aux")
+        aux = psum.tile([P, 5, P], BF16, tag="T", name="aux")
         for j in range(3):
             nc.tensor.transpose(
                 out=aux[:, j, :], in_=muni[:, P * j : P * j + P], identity=ident_b[:]
@@ -392,30 +491,33 @@ def tile_afnb_pa_kernel(tc, low_feats, wk, bk, gk, bek, mk, vk, wv, bv, out_0, o
         keep_tensor_busy()
         regroup_vector(0, 0)
         regroup_scalar(0, 0)
+        nc.vector.tensor_tensor(out=rtmp[:], in0=ident_f[:, 0:NLOC], in1=wloc[:, 0:NLOC], op=ALU.mult)
+        nc.vector.tensor_reduce(out=rs[:], in_=rtmp[:], axis=AX.X, op=ALU.add)
         keep_tensor_busy()
         pu0 = weight_transposes(w_u[:, 0, :].bitcast(F32), "U0")
         pu1 = weight_transposes(w_u[:, 1, :].bitcast(F32), "U1")
-        weight_copy(CV, pu0, False)
+        weight_copy("u", 0, pu0, False)
         quant_x(0, 0)
-        weight_copy(CV + P, pu1, True)
+        weight_copy("u", 1, pu1, True)
         keep_tensor_busy()
-        pw0 = weight_transposes(w_v[:, 0, :].bitcast(F32), "X")
-        pw1 = weight_transposes(w_v[:, 1, :].bitcast(F32), "Y")
+        pw0 = weight_transposes(w_v[:, 0, :].bitcast(F32), "A")
+        pw1 = weight_transposes(w_v[:, 1, :].bitcast(F32), "B")
         regroup_scalar(0, 1)
-        weight_quant(CV, CH)
+        weight_quant("u")
         regroup_vector(0, 1)
-        weight_copy(P, pw1, True)
         u_open(0)
         u_win(0, 0, 0, (0,))
         u_win(0, 1, 0, (0,))
-        weight_copy(0, pw0, False)
+        weight_copy("a", 0, pw0, False)
+        weight_copy("a", 1, pw1, False)
         quant_x(0, 1)
-        pbv = psum.tile([P, CV], F32, tag="T0", name="pbv")
+        pbv = psum.tile([P, CV], F32, tag="C1", name="pbv")
         nc.tensor.matmul(out=pbv[:], lhsT=ones[:], rhs=bvrow[:], start=True, stop=True)
-        pw2 = weight_transposes(w_v[:, 2, :].bitcast(F32), "Z")
+        pw2 = weight_transposes(w_v[:, 2, :].bitcast(F32), "C0")
         pw3 = weight_transposes(w_v[:, 3, :].bitcast(F32), "U2")
-        weight_copy(2 * P, pw2, False)
-        weight_copy(3 * P, pw3, True)
+        weight_copy("b", 0, pw2, True)
+        weight_copy("b", 1, pw3, True)
+        weight_quant("a")
         for k in range(2):
             nc.tensor.transpose(out=aux[:, 3 + k, :], in_=prm[:, k:256:2], identity=ident_b[:])
         u_open_tail(0)
@@ -427,66 +529,75 @@ def tile_afnb_pa_kernel(tc, low_feats, wk, bk, gk, bek, mk, vk, wv, bv, out_0, o
         u_win(0, 1, 2)
         nc.scalar.copy(out=prmt[:].rearrange("p v k -> p k v"), in_=aux[:, 3:5, 0:5])
         nc.scalar.activation(out=sc[:], in_=prmt[:, 4, :], func=ACT.Sqrt, bias=eps[:, 0:1])
-        weight_quant(0, CV)
-        nc.scalar.copy(out=bvb[:], in_=pbv[:])
+        nc.scalar.copy(out=bvb[:], in_=pbv[:, 256:512])
         nc.vector.reciprocal(out=sc[:], in_=sc[:])
         nc.gpsimd.tensor_tensor(out=bi[:], in0=prmt[:, 0, :], in1=prmt[:, 3, :], op=ALU.subtract)
         nc.gpsimd.tensor_tensor(out=sc[:], in0=sc[:], in1=prmt[:, 1, :], op=ALU.mult)
         nc.gpsimd.tensor_tensor(out=bi[:], in0=bi[:], in1=sc[:], op=ALU.mult)
         nc.gpsimd.tensor_tensor(out=bi[:], in0=bi[:], in1=prmt[:, 2, :], op=ALU.add)
-        v_mx(0, "X", 0)
-        v_mx(0, "X", 1)
-        v_mx(0, "Y", 0)
-        v_mx(0, "Y", 1)
-        v_mx(0, "Z", 0)
-        v_mx(0, "Z", 1)
-        regroup_vector(1, 0)
-        regroup_scalar(1, 0)
-        v_copy(0, "X", False)
-        quant_x(1, 0)
+        weight_quant("b")
+        px_mx(0, "X")
+        px_mx(0, "Y")
+        px_mx(0, "Z")
+        cm_mx(0, 0)
+        cm_mx(0, 1)
+        regroup_vector(1, 0, (1, 2, 3))
+        regroup_scalar(1, 0, (0,))
         u_relu(0, 0)
-        regroup_vector(1, 1)
-        regroup_scalar(1, 1)
-        v_copy(0, "Y", True)
+        quant_x(1, 0)
+        px_copy(0, "X", False)
+        px_copy_yz(0)
+        regroup_scalar(1, 1, (0, 3, 2))
+        cm_pool(0, 0)
+        regroup_vector(1, 1, (1,))
+        cm_pool(0, 1)
+        u_pool6_gpsimd(0, 0)
+        px_mx(1, "X", (0,))
+        px_mx(1, "Y", (0,))
+        px_bias(0)
+        px_pool(0, "X")
+        px_pool(0, "Y")
+        px_pool(0, "Z")
         quant_x(1, 1)
-        v_copy(0, "Z", False)
         u_relu(0, 1)
-        v_pool(0, "X")
-        v_pool(0, "Y")
+        cm_rows(0)
+        finish_px(0)
+        u_pool8(0, 0, 1)
+        u_pool6_gpsimd(0, 1)
         u_open(1)
         u_open_tail(1)
-        v_mx(1, "X", 0)
-        v_mx(1, "Y", 0)
-        v_pool(0, "Z")
+        cm_mx(1, 0)
         u_mx(1, 0)
+        cm_mx(1, 1)
         u_relu(1, 0)
+        u_pool8(0, 1, 2)
+        cm_pool(1, 0)
+        cm_total(0)
+        cm_pool(1, 1)
+        cm_rows(1)
         u_mx(1, 1)
         u_relu(1, 1)
-        v_mx(1, "Z", 0)
-        v_mx(1, "X", 1)
-        v_copy(1, "X", False)
-        v_mx(1, "Y", 1)
-        v_copy(1, "Y", False)
-        v_mx(1, "Z", 1)
-        v_copy(1, "Z", False)
-        u_pool8(0, 0, 2)
-        u_pool6(0, 0, 2)
-        u_pool31(0)
-        scale_keys(0, 8)
-        scale_keys(0, 6)
+        cm_transposes(0)
+        px_mx(1, "X", (1,))
+        px_copy(1, "X", False)
+        px_mx(1, "Y", (1,))
+        px_mx(1, "Z")
+        px_copy_yz(1)
+        finish_cm(0)
+        u_pool8(1, 0, 2)
+        px_bias(1)
+        px_pool(1, "X")
+        px_pool(1, "Y")
+        px_pool(1, "Z")
+        cm_total(1)
+        scale_keys(kov[:, :, 46:110], sums8[:].rearrange("p b k l -> p (b k) l"), 9)
+        u_pool6(1, 0, 2)
+        cm_transposes(1)
+        finish_px(1)
+        u_pool31()
+        scale_keys(kov[:, :, 10:46], sums6[:].rearrange("p b k l -> p (b k) l"), 16)
+        scale_keys(kov[:, :, 0], sums1[:], 576)
+        scale_keys(kov[:, :, 1:10], sums3[:], 64)
         store_keys(0)
-        finish_value(0, 0)
-        finish_value(0, 1)
-        u_pool8(1, 0, 1)
-        u_pool6(1, 0, 1)
-        v_pool(1, "X")
-        v_pool(1, "Y")
-        v_pool(1, "Z")
-        u_pool6(1, 1, 2)
-        u_pool8(1, 1, 2)
-        u_pool31(1)
-        scale_keys(1, 8)
-        scale_keys(1, 6)
         store_keys(1)
-        finish_value(1, 0)
-        finish_value(1, 1)
+        finish_cm(1)

@@ -62,19 +62,19 @@ def tile_afnb_pa_kernel(tc, low_feats, wk, bk, gk, bek, mk, vk, wv, bv, out_0, o
         rtmp = keep.tile([P, NLOC], F32)
         sums8 = keep.tile([P, NB, 2, 64], F32)
         sums6 = keep.tile([P, NB, 2, 36], F32)
-        half = keep.tile([P, 2 * NB, 18], F32)
-        sums3 = keep.tile([P, 2 * NB, 9], F32)
-        sums1 = keep.tile([P, 2 * NB], F32)
+        half = keep.tile([P, NB, 2, 18], F32)
+        sums3 = keep.tile([P, NB, 2, 9], F32)
+        sums1 = keep.tile([P, NB, 2], F32)
         ko = keep.tile([P, NB, 2, NLOC], F32)
         prmt = keep.tile([P, 5, 2], F32)
         eps = keep.tile([P, 1], F32)
         sc = keep.tile([P, 2], F32)
         bi = keep.tile([P, 2], F32)
         wg, wc, wsc = {}, {}, {}
-        for grp in "uab":
-            wg_t = keep.tile([P, 2048], BF16, align_bytes=64, name="wg_" + grp)
-            wc_t = keep.tile([P, 512], U32, align_bytes=64, name="wc_" + grp)
-            ws_t = keep.tile([P, 512], U8, align_bytes=64, name="ws_" + grp)
+        for grp, cols in (("u", 512), ("v", 1024)):
+            wg_t = keep.tile([P, 4 * cols], BF16, align_bytes=64, name="wg_" + grp)
+            wc_t = keep.tile([P, cols], U32, align_bytes=64, name="wc_" + grp)
+            ws_t = keep.tile([P, cols], U8, align_bytes=64, name="ws_" + grp)
             wg[grp], wc[grp], wsc[grp] = wg_t, wc_t, ws_t
         xg = keep.tile([P, 4 * CW * 4], BF16, align_bytes=64)
         xc = keep.tile([P, 4 * CW], U32, align_bytes=64)
@@ -115,8 +115,8 @@ def tile_afnb_pa_kernel(tc, low_feats, wk, bk, gk, bek, mk, vk, wv, bv, out_0, o
 
         def weight_copy(grp, k, pw, on_vector):
             words = wg[grp][:].bitcast(F32)
-            if grp == "a":
-                dst = words.rearrange("p (g k c u) -> p g k c u", g=2, k=2, u=2)[:, :, k, :, :]
+            if grp == "v":
+                dst = words.rearrange("p (g k c u) -> p g k c u", g=2, k=4, u=2)[:, :, k, :, :]
             else:
                 dst = words.rearrange("p (k g c u) -> p k g c u", k=2, g=2, u=2)[:, k, :, :, :]
             src = pw[:].rearrange("p g u c -> p g c u")
@@ -125,8 +125,9 @@ def tile_afnb_pa_kernel(tc, low_feats, wk, bk, gk, bek, mk, vk, wv, bv, out_0, o
             else:
                 nc.scalar.copy(out=dst, in_=src)
 
-        def weight_quant(grp, parts=((0, 256), (256, 512))):
-            for lo, hi in parts:
+        def weight_quant(grp, g0=0, g1=2):
+            n = wc[grp].shape[1] // 2
+            for lo, hi in [(n * g, n * g + n) for g in range(g0, g1)]:
                 nc.vector.quantize_mx(
                     out=wc[grp][:, lo:hi].bitcast(FP8X4),
                     scales=wsc[grp][:, lo:hi],
@@ -234,70 +235,73 @@ def tile_afnb_pa_kernel(tc, low_feats, wk, bk, gk, bek, mk, vk, wv, bv, out_0, o
                 )
 
         PX_PASSES = {"X": (0, 384), "Y": (128, 512), "Z": (256,)}
+        PX_COLS = (256, CV)
 
         def px_mx(b, part, gs=(0, 1)):
+            n = PX_COLS[b]
             if 0 in gs:
-                if part == "X":
-                    state["X", b] = psum.tile([P, 256], F32, tag="A", name="pxa%d" % b)
+                if b == 1:
+                    bank = psum.tile([P, CV], F32, tag={"X": "A", "Y": "B", "Z": "C0"}[part], name="px1" + part)
+                    state[part, b] = bank[:, :]
+                elif part == "X":
+                    bank = psum.tile([P, CV], F32, tag="A", name="px0X")
+                    state["X", b] = bank[:, 0:256]
                 elif part == "Y":
-                    yz = psum.tile([P, 2, 256], F32, tag="B", name="pxb%d" % b)
-                    state["Y", b] = yz[:, 0, :]
-                    state["Z", b] = yz[:, 1, :]
-            out = state[part, b]
+                    bank = psum.tile([P, CV], F32, tag="B", name="px0YZ")
+                    state["Y", b] = bank[:, 0:256]
+                    state["Z", b] = bank[:, 256:512]
             offs = PX_PASSES[part]
             for g in gs:
                 for i, off in enumerate(offs):
                     x0 = xcol(b, g) + off
                     nc.tensor.matmul_mx(
-                        out=out[:] if part == "X" else out,
+                        out=state[part, b],
                         lhsT=xc[:, x0 : x0 + P].bitcast(FP8X4),
                         lhsT_scale=xs[:, x0 : x0 + P],
-                        rhs=wc["a"][:, 256 * g : 256 * g + 256].bitcast(FP8X4),
-                        rhs_scale=wsc["a"][:, 256 * g : 256 * g + 256],
+                        rhs=wc["v"][:, CV * g : CV * g + n].bitcast(FP8X4),
+                        rhs_scale=wsc["v"][:, CV * g : CV * g + n],
                         start=(g == 0 and i == 0),
                         stop=(g == 1 and i == len(offs) - 1),
                     )
 
-        def px_copy(b, part, on_vector):
-            vsb = work.tile([P, 256], F32, tag="v" + part, name="vsb%s%d" % (part, b))
-            state["v" + part, b] = vsb
-            src = state[part, b][:] if part == "X" else state[part, b]
+        def px_copy(b, part, on_vector=False):
+            n = PX_COLS[b]
+            vsb = work.tile([P, CV], F32, tag="v" + part, name="vsb%s%d" % (part, b))
+            state["v" + part, b] = vsb[:, 0:n]
             if on_vector:
-                nc.vector.tensor_copy(out=vsb[:], in_=src)
+                nc.vector.tensor_copy(out=vsb[:, 0:n], in_=state[part, b])
             else:
-                nc.scalar.copy(out=vsb[:], in_=src)
-
-        def px_copy_yz(b):
-            vsb = work.tile([P, 2, 256], F32, tag="vYZ", name="vsbyz%d" % b)
-            nc.scalar.copy(out=vsb[:, 0, :], in_=state["Y", b])
-            nc.scalar.copy(out=vsb[:, 1, :], in_=state["Z", b])
-            state["vY", b] = vsb[:, 0, :]
-            state["vZ", b] = vsb[:, 1, :]
+                nc.scalar.copy(out=vsb[:, 0:n], in_=state[part, b])
 
         def px_bias(b):
-            state["pt", b] = psum.tile([P, CV], F32, tag="T", name="pt%d" % b)
-            nc.tensor.matmul(
-                out=state["pt", b][:, 0:256], lhsT=ones[:], rhs=bvrow[:, 0:256], start=True, stop=False
-            )
+            for h in range(PX_COLS[b] // 256):
+                pt = psum.tile([P, CV], F32, tag=("T", "C1", "U0")[b + h], name="pt%d%d" % (b, h))
+                state["pt", b, h] = pt
+                nc.tensor.matmul(
+                    out=pt[:, 0:256], lhsT=ones[:], rhs=bvrow[:, 256 * h : 256 * h + 256],
+                    start=True, stop=False,
+                )
 
         def px_pool(b, part):
-            nc.tensor.matmul(
-                out=state["pt", b][:, 0:256], lhsT=pmat[:, "XYZ".index(part), :],
-                rhs=state["v" + part, b][:], start=False, stop=(part == "Z"),
-            )
+            for h in range(PX_COLS[b] // 256):
+                nc.tensor.matmul(
+                    out=state["pt", b, h][:, 0:256], lhsT=pmat[:, "XYZ".index(part), :],
+                    rhs=state["v" + part, b][:, 256 * h : 256 * h + 256],
+                    start=False, stop=(part == "Z"),
+                )
 
         def cm_mx(b, k):
             pc = psum.tile([P, 384], F32, tag="C%d" % k, name="pc%d%d" % (b, k))
             state["pc", b, k] = pc
             for lo, n, offs in ((0, 256, (0, 384)), (256, 128, (256,))):
                 for g in range(2):
-                    w0 = P * (2 * k + g)
+                    w0 = CV * g + 256 + P * k
                     for i, off in enumerate(offs):
                         x0 = xcol(b, g) + off
                         nc.tensor.matmul_mx(
                             out=pc[:, lo : lo + n],
-                            lhsT=wc["b"][:, w0 : w0 + P].bitcast(FP8X4),
-                            lhsT_scale=wsc["b"][:, w0 : w0 + P],
+                            lhsT=wc["v"][:, w0 : w0 + P].bitcast(FP8X4),
+                            lhsT_scale=wsc["v"][:, w0 : w0 + P],
                             rhs=xc[:, x0 : x0 + n].bitcast(FP8X4),
                             rhs_scale=xs[:, x0 : x0 + n],
                             start=(g == 0 and i == 0),
@@ -348,19 +352,23 @@ def tile_afnb_pa_kernel(tc, low_feats, wk, bk, gk, bek, mk, vk, wv, bv, out_0, o
         def cm_transposes(b):
             for k in range(2):
                 nc.tensor.transpose(
-                    out=state["pt", b][:, 256 + P * k : 384 + P * k], in_=sv[:, b, k, :],
+                    out=state["pt", b, 0][:, 256 + P * k : 384 + P * k], in_=sv[:, b, k, :],
                     identity=ident_f[:],
                 )
 
-        def finish_px(b):
-            vo = work.tile([P, 256], F32, tag="vo0", name="vo0%d" % b)
-            nc.scalar.copy(out=vo[:], in_=state["pt", b][:, 0:256])
-            nc.sync.dma_start(out=out_0[b, :, 0:256], in_=vo[0:NLOC, :])
+        def finish_px(b, h, on_vector=False):
+            vo = work.tile([P, 256], F32, tag="vo%d" % h, name="vo%d%d" % (h, b))
+            src = state["pt", b, h][:, 0:256]
+            if on_vector:
+                nc.vector.tensor_copy(out=vo[:], in_=src)
+            else:
+                nc.scalar.copy(out=vo[:], in_=src)
+            nc.sync.dma_start(out=out_0[b, :, 256 * h : 256 * h + 256], in_=vo[0:NLOC, :])
 
         def finish_cm(b):
             vo = work.tile([P, 256], F32, tag="vo1", name="vo1%d" % b)
             nc.vector.scalar_tensor_tensor(
-                out=vo[:], in0=state["pt", b][:, 256:512], scalar=rs[:, 0:1],
+                out=vo[:], in0=state["pt", b, 0][:, 256:512], scalar=rs[:, 0:1],
                 in1=bvb[:], op0=ALU.mult, op1=ALU.add,
             )
             nc.sync.dma_start(out=out_0[b, :, 256:512], in_=vo[0:NLOC, :])
@@ -401,22 +409,27 @@ def tile_afnb_pa_kernel(tc, low_feats, wk, bk, gk, bek, mk, vk, wv, bv, out_0, o
                 axis=AX.XY, op=ALU.add,
             )
 
-        def u_pool31():
-            six = sums6[:].rearrange("p b k l -> p (b k) l")
+        def u_pool31(b):
+            six = sums6[:, b, :, :]
             nc.vector.tensor_reduce(
-                out=half[:], in_=six.rearrange("p a (m j) -> p a m j", j=2), axis=AX.X, op=ALU.add
+                out=half[:, b, :, :], in_=six.rearrange("p k (m j) -> p k m j", j=2),
+                axis=AX.X, op=ALU.add,
             )
-            nc.vector.tensor_reduce(out=sums1[:], in_=six, axis=AX.X, op=ALU.add)
+            nc.vector.tensor_reduce(out=sums1[:, b, :], in_=six, axis=AX.X, op=ALU.add)
             nc.vector.tensor_reduce(
-                out=sums3[:].rearrange("p a (g c) -> p (a g) c", c=3),
-                in_=half[:].rearrange("p a (g i c) -> p (a g) c i", i=2, c=3),
+                out=sums3[:, b, :, :].rearrange("p k (g c) -> p (k g) c", c=3),
+                in_=half[:, b, :, :].rearrange("p k (g i c) -> p (k g) c i", i=2, c=3),
                 axis=AX.X, op=ALU.add,
             )
 
-        kov = ko[:].rearrange("p b k l -> p (b k) l")
-
-        def scale_keys(dst, src, count):
-            nc.scalar.activation(out=dst, in_=src, func=ACT.Copy, scale=1.0 / count)
+        def scale_keys(b, grids):
+            for dst, src, count in (
+                (ko[:, b, :, 46:110], sums8[:, b, :, :], 9),
+                (ko[:, b, :, 10:46], sums6[:, b, :, :], 16),
+                (ko[:, b, :, 1:10], sums3[:, b, :, :], 64),
+                (ko[:, b, :, 0], sums1[:, b, :], 576),
+            )[grids]:
+                nc.scalar.activation(out=dst, in_=src, func=ACT.Copy, scale=1.0 / count)
 
         def store_keys(b):
             nc.sync.dma_start(out=out_1[b].rearrange("(p k) l -> p k l", k=2), in_=ko[:, b, :, :])
@@ -505,19 +518,18 @@ def tile_afnb_pa_kernel(tc, low_feats, wk, bk, gk, bek, mk, vk, wv, bv, out_0, o
         regroup_scalar(0, 1)
         weight_quant("u")
         regroup_vector(0, 1)
+        weight_copy("v", 1, pw1, True)
         u_open(0)
         u_win(0, 0, 0, (0,))
         u_win(0, 1, 0, (0,))
-        weight_copy("a", 0, pw0, False)
-        weight_copy("a", 1, pw1, False)
+        weight_copy("v", 0, pw0, False)
         quant_x(0, 1)
         pbv = psum.tile([P, CV], F32, tag="C1", name="pbv")
         nc.tensor.matmul(out=pbv[:], lhsT=ones[:], rhs=bvrow[:], start=True, stop=True)
         pw2 = weight_transposes(w_v[:, 2, :].bitcast(F32), "C0")
         pw3 = weight_transposes(w_v[:, 3, :].bitcast(F32), "U2")
-        weight_copy("b", 0, pw2, True)
-        weight_copy("b", 1, pw3, True)
-        weight_quant("a")
+        weight_copy("v", 2, pw2, False)
+        weight_copy("v", 3, pw3, True)
         for k in range(2):
             nc.tensor.transpose(out=aux[:, 3 + k, :], in_=prm[:, k:256:2], identity=ident_b[:])
         u_open_tail(0)
@@ -529,75 +541,71 @@ def tile_afnb_pa_kernel(tc, low_feats, wk, bk, gk, bek, mk, vk, wv, bv, out_0, o
         u_win(0, 1, 2)
         nc.scalar.copy(out=prmt[:].rearrange("p v k -> p k v"), in_=aux[:, 3:5, 0:5])
         nc.scalar.activation(out=sc[:], in_=prmt[:, 4, :], func=ACT.Sqrt, bias=eps[:, 0:1])
-        nc.scalar.copy(out=bvb[:], in_=pbv[:, 256:512])
+        weight_quant("v", 0, 1)
+        nc.vector.tensor_sub(out=bi[:], in0=prmt[:, 0, :], in1=prmt[:, 3, :])
         nc.vector.reciprocal(out=sc[:], in_=sc[:])
-        nc.gpsimd.tensor_tensor(out=bi[:], in0=prmt[:, 0, :], in1=prmt[:, 3, :], op=ALU.subtract)
-        nc.gpsimd.tensor_tensor(out=sc[:], in0=sc[:], in1=prmt[:, 1, :], op=ALU.mult)
-        nc.gpsimd.tensor_tensor(out=bi[:], in0=bi[:], in1=sc[:], op=ALU.mult)
-        nc.gpsimd.tensor_tensor(out=bi[:], in0=bi[:], in1=prmt[:, 2, :], op=ALU.add)
-        weight_quant("b")
+        weight_quant("v", 1, 2)
+        nc.vector.tensor_mul(out=sc[:], in0=sc[:], in1=prmt[:, 1, :])
+        nc.scalar.copy(out=bvb[:], in_=pbv[:, 256:512])
         px_mx(0, "X")
         px_mx(0, "Y")
         px_mx(0, "Z")
         cm_mx(0, 0)
         cm_mx(0, 1)
-        regroup_vector(1, 0, (1, 2, 3))
+        regroup_vector(1, 0, (1,))
+        nc.vector.tensor_mul(out=bi[:], in0=bi[:], in1=sc[:])
+        regroup_vector(1, 0, (2, 3))
+        nc.vector.tensor_add(out=bi[:], in0=bi[:], in1=prmt[:, 2, :])
         regroup_scalar(1, 0, (0,))
-        u_relu(0, 0)
+        px_copy(0, "X")
         quant_x(1, 0)
-        px_copy(0, "X", False)
-        px_copy_yz(0)
-        regroup_scalar(1, 1, (0, 3, 2))
+        regroup_scalar(1, 1, (0,))
+        px_copy(0, "Y")
+        px_copy(0, "Z")
+        regroup_scalar(1, 1, (3,))
+        regroup_vector(1, 1, (1, 2))
         cm_pool(0, 0)
-        regroup_vector(1, 1, (1,))
-        cm_pool(0, 1)
-        u_pool6_gpsimd(0, 0)
-        px_mx(1, "X", (0,))
-        px_mx(1, "Y", (0,))
+        u_relu(0, 0)
+        u_relu(0, 1)
         px_bias(0)
         px_pool(0, "X")
         px_pool(0, "Y")
         px_pool(0, "Z")
+        px_mx(1, "X", (0,))
         quant_x(1, 1)
-        u_relu(0, 1)
+        cm_pool(0, 1)
         cm_rows(0)
-        finish_px(0)
-        u_pool8(0, 0, 1)
-        u_pool6_gpsimd(0, 1)
+        finish_px(0, 0)
         u_open(1)
         u_open_tail(1)
-        cm_mx(1, 0)
         u_mx(1, 0)
-        cm_mx(1, 1)
         u_relu(1, 0)
-        u_pool8(0, 1, 2)
-        cm_pool(1, 0)
-        cm_total(0)
-        cm_pool(1, 1)
-        cm_rows(1)
+        px_mx(1, "X", (1,))
+        px_copy(1, "X")
         u_mx(1, 1)
         u_relu(1, 1)
-        cm_transposes(0)
-        px_mx(1, "X", (1,))
-        px_copy(1, "X", False)
-        px_mx(1, "Y", (1,))
+        px_mx(1, "Y")
+        px_copy(1, "Y")
         px_mx(1, "Z")
-        px_copy_yz(1)
-        finish_cm(0)
-        u_pool8(1, 0, 2)
+        px_copy(1, "Z")
+        u_pool8(0, 0, 2)
+        u_pool6(0, 0, 2)
+        scale_keys(0, slice(0, 1))
+        cm_total(0)
         px_bias(1)
         px_pool(1, "X")
         px_pool(1, "Y")
-        px_pool(1, "Z")
-        cm_total(1)
-        scale_keys(kov[:, :, 46:110], sums8[:].rearrange("p b k l -> p (b k) l"), 9)
-        u_pool6(1, 0, 2)
-        cm_transposes(1)
-        finish_px(1)
-        u_pool31()
-        scale_keys(kov[:, :, 10:46], sums6[:].rearrange("p b k l -> p (b k) l"), 16)
-        scale_keys(kov[:, :, 0], sums1[:], 576)
-        scale_keys(kov[:, :, 1:10], sums3[:], 64)
+        u_pool31(0)
+        scale_keys(0, slice(1, 4))
         store_keys(0)
+        u_pool8(1, 0, 2)
+        u_pool6(1, 0, 2)
+        scale_keys(1, slice(0, 1))
+        u_pool31(1)
+        scale_keys(1, slice(1, 4))
         store_keys(1)
-        finish_cm(1)
+        cm_transposes(0)
+        px_pool(1, "Z")
+        finish_cm(0)
+        finish_px(1, 0)
+        finish_px(1, 1, True)

@@ -53,7 +53,7 @@ def tile_afnb_pa_kernel(tc, low_feats, wk, bk, gk, bek, mk, vk, wv, bv, out_0, o
         pmat = keep.tile([P, 3, P], F32)
         wloc = keep.tile([P, P], F32)
         r4 = keep.tile([P, 4], F32)
-        bvb = keep.tile([P, 256], F32)
+        bvb = keep.tile([P, CV], F32)
         sv = keep.tile([P, NB, 2, P], F32)
         hsum = keep.tile([P, NB, 2, 96], F32)
         s0p = keep.tile([P, NB, 2, 24], F32)
@@ -61,7 +61,7 @@ def tile_afnb_pa_kernel(tc, low_feats, wk, bk, gk, bek, mk, vk, wv, bv, out_0, o
         rs = keep.tile([P, 1], F32)
         rtmp = keep.tile([P, NLOC], F32)
         sums8 = keep.tile([P, NB, 2, 64], F32)
-        sums6 = keep.tile([P, NB, 2, 36], F32)
+        sums6 = keep.tile([P, NB, 2, 40], F32)
         half = keep.tile([P, NB, 2, 18], F32)
         sums3 = keep.tile([P, NB, 2, 9], F32)
         sums1 = keep.tile([P, NB, 2], F32)
@@ -273,21 +273,16 @@ def tile_afnb_pa_kernel(tc, low_feats, wk, bk, gk, bek, mk, vk, wv, bv, out_0, o
             else:
                 nc.scalar.copy(out=vsb[:, 0:n], in_=state[part, b])
 
-        def px_bias(b):
-            for h in range(PX_COLS[b] // 256):
-                pt = psum.tile([P, CV], F32, tag=("T", "C1", "U0")[b + h], name="pt%d%d" % (b, h))
-                state["pt", b, h] = pt
-                nc.tensor.matmul(
-                    out=pt[:, 0:256], lhsT=ones[:], rhs=bvrow[:, 256 * h : 256 * h + 256],
-                    start=True, stop=False,
-                )
-
         def px_pool(b, part):
             for h in range(PX_COLS[b] // 256):
+                if part == "X":
+                    state["pt", b, h] = psum.tile(
+                        [P, CV], F32, tag=("T", "C1", "U0")[b + h], name="pt%d%d" % (b, h)
+                    )
                 nc.tensor.matmul(
                     out=state["pt", b, h][:, 0:256], lhsT=pmat[:, "XYZ".index(part), :],
                     rhs=state["v" + part, b][:, 256 * h : 256 * h + 256],
-                    start=False, stop=(part == "Z"),
+                    start=(part == "X"), stop=(part == "Z"),
                 )
 
         def cm_mx(b, k):
@@ -356,20 +351,18 @@ def tile_afnb_pa_kernel(tc, low_feats, wk, bk, gk, bek, mk, vk, wv, bv, out_0, o
                     identity=ident_f[:],
                 )
 
-        def finish_px(b, h, on_vector=False):
+        def finish_px(b, h):
             vo = work.tile([P, 256], F32, tag="vo%d" % h, name="vo%d%d" % (h, b))
-            src = state["pt", b, h][:, 0:256]
-            if on_vector:
-                nc.vector.tensor_copy(out=vo[:], in_=src)
-            else:
-                nc.scalar.copy(out=vo[:], in_=src)
+            nc.vector.tensor_tensor(
+                out=vo[:], in0=state["pt", b, h][:, 0:256], in1=bvb[:, 256 * h : 256 * h + 256], op=ALU.add
+            )
             nc.sync.dma_start(out=out_0[b, :, 256 * h : 256 * h + 256], in_=vo[0:NLOC, :])
 
         def finish_cm(b):
             vo = work.tile([P, 256], F32, tag="vo1", name="vo1%d" % b)
             nc.vector.scalar_tensor_tensor(
                 out=vo[:], in0=state["pt", b, 0][:, 256:512], scalar=rs[:, 0:1],
-                in1=bvb[:], op0=ALU.mult, op1=ALU.add,
+                in1=bvb[:, 256:512], op0=ALU.mult, op1=ALU.add,
             )
             nc.sync.dma_start(out=out_0[b, :, 256:512], in_=vo[0:NLOC, :])
 
@@ -387,7 +380,7 @@ def tile_afnb_pa_kernel(tc, low_feats, wk, bk, gk, bek, mk, vk, wv, bv, out_0, o
             nc.gpsimd.tensor_tensor(out=h6[:], in0=p6bv[:, :, 0, :], in1=p6bv[:, :, 1, :], op=ALU.add)
             h6v = h6[:].rearrange("p (g a) c -> p g a c", a=2)
             nc.gpsimd.tensor_tensor(
-                out=sums6[:, b, k, :].rearrange("p (g c) -> p g c", c=6),
+                out=sums6[:, b, k, 0:36].rearrange("p (g c) -> p g c", c=6),
                 in0=h6v[:, :, 0, :], in1=h6v[:, :, 1, :], op=ALU.add,
             )
 
@@ -400,17 +393,15 @@ def tile_afnb_pa_kernel(tc, low_feats, wk, bk, gk, bek, mk, vk, wv, bv, out_0, o
                 axis=AX.XY, op=ALU.add,
             )
 
-        def u_pool6(b, k0, k1):
+        def u_pool6(b, k):
             nc.vector.tensor_reduce(
-                out=sums6[:, b, k0:k1, :].rearrange("p k (g c) -> p (k g) c", c=6),
-                in_=state["r", b][:, k0:k1, :].rearrange(
-                    "p k (g i c j) -> p (k g) c i j", i=4, c=6, j=4
-                ),
+                out=sums6[:, b, k, 0:36].rearrange("p (g c) -> p g c", c=6),
+                in_=state["r", b][:, k, :].rearrange("p (g i c j) -> p g c i j", i=4, c=6, j=4),
                 axis=AX.XY, op=ALU.add,
             )
 
         def u_pool31(b):
-            six = sums6[:, b, :, :]
+            six = sums6[:, b, :, 0:36]
             nc.vector.tensor_reduce(
                 out=half[:, b, :, :], in_=six.rearrange("p k (m j) -> p k m j", j=2),
                 axis=AX.X, op=ALU.add,
@@ -425,7 +416,7 @@ def tile_afnb_pa_kernel(tc, low_feats, wk, bk, gk, bek, mk, vk, wv, bv, out_0, o
         def scale_keys(b, grids):
             for dst, src, count in (
                 (ko[:, b, :, 46:110], sums8[:, b, :, :], 9),
-                (ko[:, b, :, 10:46], sums6[:, b, :, :], 16),
+                (ko[:, b, :, 10:46], sums6[:, b, :, 0:36], 16),
                 (ko[:, b, :, 1:10], sums3[:, b, :, :], 64),
                 (ko[:, b, :, 0], sums1[:, b, :], 576),
             )[grids]:
@@ -506,7 +497,6 @@ def tile_afnb_pa_kernel(tc, low_feats, wk, bk, gk, bek, mk, vk, wv, bv, out_0, o
         regroup_scalar(0, 0)
         nc.vector.tensor_tensor(out=rtmp[:], in0=ident_f[:, 0:NLOC], in1=wloc[:, 0:NLOC], op=ALU.mult)
         nc.vector.tensor_reduce(out=rs[:], in_=rtmp[:], axis=AX.X, op=ALU.add)
-        keep_tensor_busy()
         pu0 = weight_transposes(w_u[:, 0, :].bitcast(F32), "U0")
         pu1 = weight_transposes(w_u[:, 1, :].bitcast(F32), "U1")
         weight_copy("u", 0, pu0, False)
@@ -546,7 +536,7 @@ def tile_afnb_pa_kernel(tc, low_feats, wk, bk, gk, bek, mk, vk, wv, bv, out_0, o
         nc.vector.reciprocal(out=sc[:], in_=sc[:])
         weight_quant("v", 1, 2)
         nc.vector.tensor_mul(out=sc[:], in0=sc[:], in1=prmt[:, 1, :])
-        nc.scalar.copy(out=bvb[:], in_=pbv[:, 256:512])
+        nc.scalar.copy(out=bvb[:], in_=pbv[:])
         px_mx(0, "X")
         px_mx(0, "Y")
         px_mx(0, "Z")
@@ -567,7 +557,6 @@ def tile_afnb_pa_kernel(tc, low_feats, wk, bk, gk, bek, mk, vk, wv, bv, out_0, o
         cm_pool(0, 0)
         u_relu(0, 0)
         u_relu(0, 1)
-        px_bias(0)
         px_pool(0, "X")
         px_pool(0, "Y")
         px_pool(0, "Z")
@@ -575,7 +564,7 @@ def tile_afnb_pa_kernel(tc, low_feats, wk, bk, gk, bek, mk, vk, wv, bv, out_0, o
         quant_x(1, 1)
         cm_pool(0, 1)
         cm_rows(0)
-        finish_px(0, 0)
+        u_pool6_gpsimd(0, 0)
         u_open(1)
         u_open_tail(1)
         u_mx(1, 0)
@@ -588,24 +577,26 @@ def tile_afnb_pa_kernel(tc, low_feats, wk, bk, gk, bek, mk, vk, wv, bv, out_0, o
         px_copy(1, "Y")
         px_mx(1, "Z")
         px_copy(1, "Z")
+        finish_px(0, 0)
         u_pool8(0, 0, 2)
-        u_pool6(0, 0, 2)
-        scale_keys(0, slice(0, 1))
+        u_pool8(1, 0, 1)
+        u_pool6(1, 0)
         cm_total(0)
-        px_bias(1)
         px_pool(1, "X")
         px_pool(1, "Y")
-        u_pool31(0)
-        scale_keys(0, slice(1, 4))
-        store_keys(0)
-        u_pool8(1, 0, 2)
-        u_pool6(1, 0, 2)
+        u_pool6(1, 1)
+        u_pool8(1, 1, 2)
         scale_keys(1, slice(0, 1))
         u_pool31(1)
         scale_keys(1, slice(1, 4))
         store_keys(1)
+        scale_keys(0, slice(0, 1))
+        u_pool6(0, 1)
+        u_pool31(0)
+        scale_keys(0, slice(1, 4))
+        store_keys(0)
         cm_transposes(0)
         px_pool(1, "Z")
         finish_cm(0)
         finish_px(1, 0)
-        finish_px(1, 1, True)
+        finish_px(1, 1)

@@ -548,12 +548,12 @@ def tile_afnb_pa_kernel(tc, low_feats, wk, bk, gk, bek, mk, vk, wv, bv, out_0, o
         nc.vector.tensor_add(out=bi[:], in0=bi[:], in1=prmt[:, 2, :])
         regroup_scalar(1, 0, (0,))
         px_copy(0, "X")
-        quant_x(1, 0)
         regroup_scalar(1, 1, (0,))
         px_copy(0, "Y")
         px_copy(0, "Z")
         regroup_scalar(1, 1, (3,))
         regroup_vector(1, 1, (1, 2))
+        quant_x(1, 0)
         cm_pool(0, 0)
         u_relu(0, 0)
         u_relu(0, 1)
@@ -564,7 +564,6 @@ def tile_afnb_pa_kernel(tc, low_feats, wk, bk, gk, bek, mk, vk, wv, bv, out_0, o
         quant_x(1, 1)
         cm_pool(0, 1)
         cm_rows(0)
-        u_pool6_gpsimd(0, 0)
         u_open(1)
         u_open_tail(1)
         u_mx(1, 0)
@@ -577,10 +576,15 @@ def tile_afnb_pa_kernel(tc, low_feats, wk, bk, gk, bek, mk, vk, wv, bv, out_0, o
         px_copy(1, "Y")
         px_mx(1, "Z")
         px_copy(1, "Z")
-        finish_px(0, 0)
+        u_pool6(0, 0)
+        u_pool6(0, 1)
         u_pool8(0, 0, 2)
-        u_pool8(1, 0, 1)
+        finish_px(0, 0)
+        u_pool31(0)
+        scale_keys(0, slice(0, 4))
+        store_keys(0)
         u_pool6(1, 0)
+        u_pool8(1, 0, 1)
         cm_total(0)
         px_pool(1, "X")
         px_pool(1, "Y")
@@ -590,11 +594,6 @@ def tile_afnb_pa_kernel(tc, low_feats, wk, bk, gk, bek, mk, vk, wv, bv, out_0, o
         u_pool31(1)
         scale_keys(1, slice(1, 4))
         store_keys(1)
-        scale_keys(0, slice(0, 1))
-        u_pool6(0, 1)
-        u_pool31(0)
-        scale_keys(0, slice(1, 4))
-        store_keys(0)
         cm_transposes(0)
         px_pool(1, "Z")
         finish_cm(0)

from contextlib import ExitStack

import concourse.mybir as mybir
from concourse.masks import make_identity

F32 = mybir.dt.float32
BF16 = mybir.dt.bfloat16
U32 = mybir.dt.uint32
U8 = mybir.dt.uint8
FP8X4 = mybir.dt.float8_e4m3fn_x4
ALU = mybir.AluOpType
ACT = mybir.ActivationFunctionType
AX = mybir.AxisListType

P = 128
NB = 2
NPX = 576
CW = 640
CV = 512
NLOC = 110
EPS = 1e-5
FLOPS = 2 * 768 * 1024 * 1152


def tile_afnb_pa_kernel(tc, low_feats, wk, bk, gk, bek, mk, vk, wv, bv, out_0, out_1):
    nc = tc.nc
    with ExitStack() as ctx:
        keep = ctx.enter_context(tc.tile_pool(name="keep", bufs=1))
        work = ctx.enter_context(tc.tile_pool(name="work", bufs=2))
        psum = ctx.enter_context(tc.psum_pool(name="psum", bufs=1))
        ctx.enter_context(tc.manual_schedule())

        prm = keep.tile([P, 256], BF16)
        bvrow = keep.tile([P, CV], BF16)
        ones = keep.tile([P, P], BF16)
        w_u = keep.tile([P, 2, 1024], BF16)
        w_v = keep.tile([P, 4, 1024], BF16)
        xr = []
        for b in range(NB):
            row = []
            for g in range(2):
                xr_bg = keep.tile([P, 4, NPX], BF16, name="xr%d%d" % (b, g))
                row.append(xr_bg)
            xr.append(row)
        ident_b = keep.tile([P, P], BF16)
        busy_in = keep.tile([P, 256], F32)
        ident_f = keep.tile([P, P], F32)
        warm = keep.tile([P, 1], F32)
        q8 = keep.tile([P, 8, 24], BF16)
        q6 = keep.tile([P, 6, 24], BF16)
        q3 = keep.tile([P, 3, 24], BF16)
        muni = keep.tile([P, 384], BF16)
        pmat = keep.tile([P, 3, P], F32)
        wloc = keep.tile([P, P], F32)
        r4 = keep.tile([P, 4], F32)
        bvb = keep.tile([P, CV], F32)
        sv = keep.tile([P, NB, 2, P], F32)
        hsum = keep.tile([P, NB, 2, 96], F32)
        s0p = keep.tile([P, NB, 2, 24], F32)
        vhalf = keep.tile([P, NB, 2, 18], F32)
        rs = keep.tile([P, 1], F32)
        rtmp = keep.tile([P, NLOC], F32)
        sums8 = keep.tile([P, NB, 2, 64], F32)
        sums6 = keep.tile([P, NB, 2, 40], F32)
        half = keep.tile([P, NB, 2, 18], F32)
        sums3 = keep.tile([P, NB, 2, 9], F32)
        sums1 = keep.tile([P, NB, 2], F32)
        ko = keep.tile([P, NB, 2, NLOC], F32)
        prmt = keep.tile([P, 5, 2], F32)
        eps = keep.tile([P, 1], F32)
        sc = keep.tile([P, 2], F32)
        bi = keep.tile([P, 2], F32)
        wg, wc, wsc = {}, {}, {}
        for grp, cols in (("u", 512), ("v", 1024)):
            wg_t = keep.tile([P, 4 * cols], BF16, align_bytes=64, name="wg_" + grp)
            wc_t = keep.tile([P, cols], U32, align_bytes=64, name="wc_" + grp)
            ws_t = keep.tile([P, cols], U8, align_bytes=64, name="ws_" + grp)
            wg[grp], wc[grp], wsc[grp] = wg_t, wc_t, ws_t
        xg = keep.tile([P, 4 * CW * 4], BF16, align_bytes=64)
        xc = keep.tile([P, 4 * CW], U32, align_bytes=64)
        xs = keep.tile([P, 4 * CW], U8, align_bytes=64)

        def load_x(b, g):
            nc.sync.dma_start(
                out=xr[b][g][:],
                in_=low_feats[b, 512 * g : 512 * g + 512].rearrange("(q t) h w -> q t (h w)", t=4),
            )

        def load_wk(k):
            nc.sync.dma_start(
                out=w_u[:, k, :], in_=wk.rearrange("(p k) c -> p k c", k=2)[:, k, :]
            )

        def load_wv(r0):
            nc.sync.dma_start(
                out=w_v[:, r0 : r0 + 2, :],
                in_=wv[P * r0 : P * r0 + 256, :].rearrange("(r p) k -> p r k", p=P),
            )

        def keep_tensor_busy():
            nc.tensor.matmul(
                out=busy_out[:], lhsT=ident_f[:], rhs=busy_in[:], start=True, stop=True
            )

        def weight_transposes(words, bank):
            pw = psum.tile([P, 2, 2, P], F32, tag=bank, name="pw_" + bank)
            for g in range(2):
                for u in range(2):
                    nc.tensor.transpose(
                        out=pw[:, g, u, :],
                        in_=words[:, 256 * g + u : 256 * g + 256 : 2],
                        identity=ident_f[:],
                    )
            return pw

        def weight_copy(grp, k, pw, on_vector):
            words = wg[grp][:].bitcast(F32)
            if grp == "v":
                dst = words.rearrange("p (g k c u) -> p g k c u", g=2, k=4, u=2)[:, :, k, :, :]
            else:
                dst = words.rearrange("p (k g c u) -> p k g c u", k=2, g=2, u=2)[:, k, :, :, :]
            src = pw[:].rearrange("p g u c -> p g c u")
            if on_vector:
                nc.vector.tensor_copy(out=dst, in_=src)
            else:
                nc.scalar.copy(out=dst, in_=src)

        def weight_quant(grp, g0=0, g1=2):
            n = wc[grp].shape[1] // 2
            for lo, hi in [(n * g, n * g + n) for g in range(g0, g1)]:
                nc.vector.quantize_mx(
                    out=wc[grp][:, lo:hi].bitcast(FP8X4),
                    scales=wsc[grp][:, lo:hi],
                    in_=wg[grp][:, 4 * lo : 4 * hi],
                )

        def xcol(b, g):
            return (2 * b + g) * CW

        def regroup(b, g, part, copy):
            base = xcol(b, g)
            if part == 1:
                dst = xg[:, 4 * base : 4 * (base + 192)].rearrange(
                    "p (m c i t) -> p m c t i", m=8, i=4, t=4
                )
                src = xr[b][g][:].rearrange("p t (m c i) -> p m c t i", m=8, i=4)[:, :, 6:12, :, :]
            elif part == 0:
                dst = xg[:, 4 * (base + 192) : 4 * (base + 384)].rearrange(
                    "p (q c i t) -> p q c t i", q=4, i=4, t=4
                )
                src = xr[b][g][:].rearrange("p t (q c i) -> p q c t i", q=4, i=4)[:, :, 12:24, :, :]
            else:
                w = part - 2
                dst = xg[:, 4 * (base + 384) : 4 * (base + 576)].rearrange(
                    "p (q w c i t) -> p q w c t i", q=4, w=2, i=4, t=4
                )[:, :, w, :, :, :]
                src = xr[b][g][:].rearrange("p t (q c i) -> p q c t i", q=4, i=4)[
                    :, :, 30 * w : 30 * w + 6, :, :
                ]
            copy(out=dst, in_=src)

        def regroup_vector(b, g, parts=(1, 2)):
            for part in parts:
                regroup(b, g, part, nc.vector.tensor_copy)

        def regroup_scalar(b, g, parts=(0, 3)):
            for part in parts:
                regroup(b, g, part, nc.scalar.copy)

        def quant_x(b, g):
            for lo, hi in ((0, 512), (512, 640)):
                lo += xcol(b, g)
                hi += xcol(b, g)
                nc.vector.quantize_mx(
                    out=xc[:, lo:hi].bitcast(FP8X4),
                    scales=xs[:, lo:hi],
                    in_=xg[:, 4 * lo : 4 * hi],
                )

        state = {}

        def u_open(b):
            for k in range(2):
                state["pu", b, k] = psum.tile([P, 384], F32, tag="U%d" % k, name="pu%d_%d" % (k, b))

        def u_open_tail(b):
            state["pu", b, 2] = psum.tile([P, 2, 256], F32, tag="U2", name="pu2_%d" % b)

        def u_win(b, k, win, gs=(0, 1)):
            if win < 2:
                lo, n = ((0, 256), (256, 128))[win]
                out = state["pu", b, k][:, lo : lo + n]
            else:
                lo, n = 384, 256
                out = state["pu", b, 2][:, k, :]
            for g in gs:
                x0 = xcol(b, g) + lo
                w0 = P * (2 * k + g)
                nc.tensor.matmul_mx(
                    out=out,
                    lhsT=wc["u"][:, w0 : w0 + P].bitcast(FP8X4),
                    lhsT_scale=wsc["u"][:, w0 : w0 + P],
                    rhs=xc[:, x0 : x0 + n].bitcast(FP8X4),
                    rhs_scale=xs[:, x0 : x0 + n],
                    start=(g == 0),
                    stop=(g == 1),
                )

        def u_mx(b, k):
            for win in range(3):
                u_win(b, k, win)

        def u_relu(b, k):
            if k == 0:
                state["r", b] = work.tile([P, 2, NPX], F32, tag="r_sb", name="r_sb%d" % b)
            r_k = state["r", b][:, k, :]
            pu = state["pu", b, k]
            pu2 = state["pu", b, 2]
            for dst, src in (
                (
                    r_k.rearrange("p (m r w) -> p m r w", m=8, r=3)[:, :, 1, :],
                    pu[:, 0:192].rearrange("p (m w) -> p m w", m=8),
                ),
                (
                    r_k.rearrange("p (q v) -> p q v", q=4)[:, :, 48:96],
                    pu[:, 192:384].rearrange("p (q v) -> p q v", q=4),
                ),
                (
                    r_k.rearrange("p (q r w) -> p q r w", q=4, r=6)[:, :, 0:6:5, :],
                    pu2[:, k, 0:192].rearrange("p (q r w) -> p q r w", q=4, r=2),
                ),
            ):
                nc.scalar.activation(
                    out=dst, in_=src, func=ACT.Relu, bias=bi[:, k : k + 1], scale=sc[:, k : k + 1]
                )

        PX_PASSES = {"X": (0, 384), "Y": (128, 512), "Z": (256,)}
        PX_COLS = (256, CV)

        def px_mx(b, part, gs=(0, 1)):
            n = PX_COLS[b]
            if 0 in gs:
                if b == 1:
                    bank = psum.tile([P, CV], F32, tag={"X": "A", "Y": "B", "Z": "C0"}[part], name="px1" + part)
                    state[part, b] = bank[:, :]
                elif part == "X":
                    bank = psum.tile([P, CV], F32, tag="A", name="px0X")
                    state["X", b] = bank[:, 0:256]
                elif part == "Y":
                    bank = psum.tile([P, CV], F32, tag="B", name="px0YZ")
                    state["Y", b] = bank[:, 0:256]
                    state["Z", b] = bank[:, 256:512]
            offs = PX_PASSES[part]
            for g in gs:
                for i, off in enumerate(offs):
                    x0 = xcol(b, g) + off
                    nc.tensor.matmul_mx(
                        out=state[part, b],
                        lhsT=xc[:, x0 : x0 + P].bitcast(FP8X4),
                        lhsT_scale=xs[:, x0 : x0 + P],
                        rhs=wc["v"][:, CV * g : CV * g + n].bitcast(FP8X4),
                        rhs_scale=wsc["v"][:, CV * g : CV * g + n],
                        start=(g == 0 and i == 0),
                        stop=(g == 1 and i == len(offs) - 1),
                    )

        def px_copy(b, part, on_vector=False):
            n = PX_COLS[b]
            vsb = work.tile([P, CV], F32, tag="v" + part, name="vsb%s%d" % (part, b))
            state["v" + part, b] = vsb[:, 0:n]
            if on_vector:
                nc.vector.tensor_copy(out=vsb[:, 0:n], in_=state[part, b])
            else:
                nc.scalar.copy(out=vsb[:, 0:n], in_=state[part, b])

        def px_pool(b, part):
            for h in range(PX_COLS[b] // 256):
                if part == "X":
                    state["pt", b, h] = psum.tile(
                        [P, CV], F32, tag=("T", "C1", "U0")[b + h], name="pt%d%d" % (b, h)
                    )
                nc.tensor.matmul(
                    out=state["pt", b, h][:, 0:256], lhsT=pmat[:, "XYZ".index(part), :],
                    rhs=state["v" + part, b][:, 256 * h : 256 * h + 256],
                    start=(part == "X"), stop=(part == "Z"),
                )

        def cm_mx(b, k):
            pc = psum.tile([P, 384], F32, tag="C%d" % k, name="pc%d%d" % (b, k))
            state["pc", b, k] = pc
            for lo, n, offs in ((0, 256, (0, 384)), (256, 128, (256,))):
                for g in range(2):
                    w0 = CV * g + 256 + P * k
                    for i, off in enumerate(offs):
                        x0 = xcol(b, g) + off
                        nc.tensor.matmul_mx(
                            out=pc[:, lo : lo + n],
                            lhsT=wc["v"][:, w0 : w0 + P].bitcast(FP8X4),
                            lhsT_scale=wsc["v"][:, w0 : w0 + P],
                            rhs=xc[:, x0 : x0 + n].bitcast(FP8X4),
                            rhs_scale=xs[:, x0 : x0 + n],
                            start=(g == 0 and i == 0),
                            stop=(g == 1 and i == len(offs) - 1),
                        )

        def cm_pool(b, k):
            pc = state["pc", b, k]
            nc.vector.tensor_reduce(
                out=sv[:, b, k, 46:110], in_=pc[:].rearrange("p (t a j) -> p a t j", t=2, j=3),
                axis=AX.XY, op=ALU.add,
            )
            nc.vector.tensor_reduce(
                out=hsum[:, b, k, :], in_=pc[:].rearrange("p (a j) -> p a j", j=4),
                axis=AX.X, op=ALU.add,
            )

        def cm_rows(b):
            add = ALU.add
            rows = hsum[:, b, :, :].rearrange("p k (r c) -> p k r c", c=6)
            six = sv[:, b, :, 10:46].rearrange("p k (r c) -> p k r c", c=6)
            pair = s0p[:, b, :, :].rearrange("p k (a c) -> p k a c", c=6)
            nc.gpsimd.tensor_tensor(
                out=pair, in0=rows[:, :, 8:16:2, :], in1=rows[:, :, 9:16:2, :], op=add
            )
            nc.gpsimd.tensor_tensor(
                out=six[:, :, 1:6:3, :], in0=rows[:, :, 1:8:4, :], in1=rows[:, :, 2:8:4, :], op=add
            )
            for h in range(2):
                nc.gpsimd.tensor_tensor(
                    out=six[:, :, 3 * h : 3 * h + 3 : 2, :], in0=rows[:, :, 4 * h : 4 * h + 4 : 3, :],
                    in1=pair[:, :, 2 * h : 2 * h + 2, :], op=add,
                )
            halves = vhalf[:, b, :, :].rearrange("p k (m c) -> p k m c", c=3)
            nc.gpsimd.tensor_tensor(
                out=vhalf[:, b, :, :], in0=sv[:, b, :, 10:46:2], in1=sv[:, b, :, 11:46:2], op=add
            )
            nc.gpsimd.tensor_tensor(
                out=sv[:, b, :, 1:10].rearrange("p k (g c) -> p k g c", c=3),
                in0=halves[:, :, 0:6:2, :], in1=halves[:, :, 1:6:2, :], op=add,
            )

        def cm_total(b):
            nc.vector.tensor_reduce(
                out=sv[:, b, :, 0:1], in_=sv[:, b, :, 1:10], axis=AX.X, op=ALU.add
            )

        def cm_transposes(b):
            for k in range(2):
                nc.tensor.transpose(
                    out=state["pt", b, 0][:, 256 + P * k : 384 + P * k], in_=sv[:, b, k, :],
                    identity=ident_f[:],
                )

        def finish_px(b, h):
            vo = work.tile([P, 256], F32, tag="vo%d" % h, name="vo%d%d" % (h, b))
            nc.vector.tensor_tensor(
                out=vo[:], in0=state["pt", b, h][:, 0:256], in1=bvb[:, 256 * h : 256 * h + 256], op=ALU.add
            )
            nc.sync.dma_start(out=out_0[b, :, 256 * h : 256 * h + 256], in_=vo[0:NLOC, :])

        def finish_cm(b):
            vo = work.tile([P, 256], F32, tag="vo1", name="vo1%d" % b)
            nc.vector.scalar_tensor_tensor(
                out=vo[:], in0=state["pt", b, 0][:, 256:512], scalar=rs[:, 0:1],
                in1=bvb[:, 256:512], op0=ALU.mult, op1=ALU.add,
            )
            nc.sync.dma_start(out=out_0[b, :, 256:512], in_=vo[0:NLOC, :])

        def u_pool6_gpsimd(b, k):
            r_k = state["r", b][:, k, :]
            tg = "%d%d" % (b, k)
            rv2 = r_k.rearrange("p (m j) -> p m j", j=2)
            p6 = work.tile([P, 288], F32, tag="p6", name="p6_" + tg)
            nc.gpsimd.tensor_tensor(out=p6[:], in0=rv2[:, :, 0], in1=rv2[:, :, 1], op=ALU.add)
            p6v = p6[:].rearrange("p (m j) -> p m j", j=2)
            p6b = work.tile([P, 144], F32, tag="p6b", name="p6b_" + tg)
            nc.gpsimd.tensor_tensor(out=p6b[:], in0=p6v[:, :, 0], in1=p6v[:, :, 1], op=ALU.add)
            p6bv = p6b[:].rearrange("p (a e c) -> p a e c", e=2, c=6)
            h6 = work.tile([P, 12, 6], F32, tag="h6", name="h6_" + tg)
            nc.gpsimd.tensor_tensor(out=h6[:], in0=p6bv[:, :, 0, :], in1=p6bv[:, :, 1, :], op=ALU.add)
            h6v = h6[:].rearrange("p (g a) c -> p g a c", a=2)
            nc.gpsimd.tensor_tensor(
                out=sums6[:, b, k, 0:36].rearrange("p (g c) -> p g c", c=6),
                in0=h6v[:, :, 0, :], in1=h6v[:, :, 1, :], op=ALU.add,
            )

        def u_pool8(b, k0, k1):
            nc.vector.tensor_reduce(
                out=sums8[:, b, k0:k1, :].rearrange("p k (g c) -> p (k g) c", c=8),
                in_=state["r", b][:, k0:k1, :].rearrange(
                    "p k (g i c j) -> p (k g) c i j", i=3, c=8, j=3
                ),
                axis=AX.XY, op=ALU.add,
            )

        def u_pool6(b, k):
            nc.vector.tensor_reduce(
                out=sums6[:, b, k, 0:36].rearrange("p (g c) -> p g c", c=6),
                in_=state["r", b][:, k, :].rearrange("p (g i c j) -> p g c i j", i=4, c=6, j=4),
                axis=AX.XY, op=ALU.add,
            )

        def u_pool31(b):
            six = sums6[:, b, :, 0:36]
            nc.vector.tensor_reduce(
                out=half[:, b, :, :], in_=six.rearrange("p k (m j) -> p k m j", j=2),
                axis=AX.X, op=ALU.add,
            )
            nc.vector.tensor_reduce(out=sums1[:, b, :], in_=six, axis=AX.X, op=ALU.add)
            nc.vector.tensor_reduce(
                out=sums3[:, b, :, :].rearrange("p k (g c) -> p (k g) c", c=3),
                in_=half[:, b, :, :].rearrange("p k (g i c) -> p (k g) c i", i=2, c=3),
                axis=AX.X, op=ALU.add,
            )

        def scale_keys(b, grids):
            for dst, src, count in (
                (ko[:, b, :, 46:110], sums8[:, b, :, :], 9),
                (ko[:, b, :, 10:46], sums6[:, b, :, 0:36], 16),
                (ko[:, b, :, 1:10], sums3[:, b, :, :], 64),
                (ko[:, b, :, 0], sums1[:, b, :], 576),
            )[grids]:
                nc.scalar.activation(out=dst, in_=src, func=ACT.Copy, scale=1.0 / count)

        def store_keys(b):
            nc.sync.dma_start(out=out_1[b].rearrange("(p k) l -> p k l", k=2), in_=ko[:, b, :, :])

        nc.vector.memset(bvrow[:], 0.0)
        nc.vector.memset(warm[:], 1.0)
        nc.vector.memset(prm[:], 0.0)
        nc.vector.memset(busy_in[:], 1.0)
        nc.vector.memset(sv[:, :, :, NLOC:P], 0.0)
        load_x(0, 0)
        nc.sync.dma_start(out=w_u[:], in_=wk.rearrange("(p k) c -> p k c", k=2))
        load_wv(0)
        nc.sync.dma_start(out=bvrow[0:1, :], in_=bv.rearrange("(o c) -> o c", o=1))
        load_x(0, 1)
        load_wv(2)
        load_x(1, 0)
        for i, vec in enumerate((bk, gk, bek, mk, vk)):
            nc.sync.dma_start(out=prm[i : i + 1, :], in_=vec.rearrange("(o c) -> o c", o=1))
        load_x(1, 1)
        nc.scalar.activation(out=warm[:], in_=warm[:], func=ACT.Sqrt)
        for i, count in enumerate((576.0, 64.0, 16.0, 9.0)):
            nc.gpsimd.memset(r4[:, i : i + 1], count)
        make_identity(nc, ident_b[:])
        make_identity(nc, ident_f[:])
        nc.gpsimd.memset(ones[:], 1.0)
        nc.gpsimd.memset(eps[:], EPS)
        nc.gpsimd.memset(xg[:].rearrange("p (a c) -> p a c", a=4)[:, :, 4 * NPX : 4 * CW], 0.0)
        for qt, off, grid, bs in ((q8, 46, 8, 3), (q6, 10, 6, 4), (q3, 1, 3, 8)):
            nc.vector.tensor_copy(
                out=qt[:].rearrange("p g (c j) -> p g c j", j=bs),
                in_=ident_b[:, off : off + grid * grid]
                .rearrange("p (g c) -> p g c", c=grid)
                .unsqueeze(3)
                .to_broadcast([P, grid, grid, bs]),
            )
        nc.vector.reciprocal(out=r4[:], in_=r4[:])
        q6r = q6[:].rearrange("p (g i) w -> p g i w", i=2)
        nc.vector.tensor_scalar_add(out=q3[:], in0=q3[:], scalar1=ident_f[:, 0:1])
        nc.vector.tensor_tensor(
            out=q6r, in0=q6r, in1=q3[:].unsqueeze(2).to_broadcast([P, 3, 2, 24]), op=ALU.add
        )
        m12 = muni[:, 0:192].rearrange("p (h a v) -> p h a v", h=2, a=2)
        q8a = q8[:].rearrange("p (h a b) w -> p h a (b w)", h=2, a=2)
        q6h = q6[:].rearrange("p (h r) w -> p h (r w)", h=2)
        for a in range(2):
            nc.vector.tensor_tensor(
                out=m12[:, :, a, :], in0=q8a[:, :, a, :], in1=q6h[:, :, 24 * a : 24 * a + 48], op=ALU.add
            )
        m0 = muni[:, 192:384].rearrange("p (a b w) -> p a b w", a=4, b=2)
        q8b = q8[:].rearrange("p (a b) w -> p a b w", a=4)
        for h in range(2):
            nc.vector.tensor_tensor(
                out=m0[:, 2 * h : 2 * h + 2, :, :],
                in0=q8b[:, 2 * h : 2 * h + 2, :, :],
                in1=q6[:, 3 * h : 3 * h + 3 : 2, :].unsqueeze(2).to_broadcast([P, 2, 2, 24]),
                op=ALU.add,
            )
        for i, (lo, hi) in enumerate(((0, 1), (1, 10), (10, 46), (46, P))):
            nc.vector.tensor_copy(
                out=wloc[:, lo:hi], in_=r4[:, i : i + 1].to_broadcast([P, hi - lo])
            )
        busy_out = psum.tile([P, 256], F32, tag="C0", name="busy_out")
        keep_tensor_busy()
        aux = psum.tile([P, 5, P], BF16, tag="T", name="aux")
        for j in range(3):
            nc.tensor.transpose(
                out=aux[:, j, :], in_=muni[:, P * j : P * j + P], identity=ident_b[:]
            )
        nc.vector.tensor_tensor(
            out=pmat[:], in0=aux[:, 0:3, :], in1=wloc[:].unsqueeze(1).to_broadcast([P, 3, P]), op=ALU.mult
        )
        keep_tensor_busy()
        regroup_vector(0, 0)
        regroup_scalar(0, 0)
        nc.vector.tensor_tensor(out=rtmp[:], in0=ident_f[:, 0:NLOC], in1=wloc[:, 0:NLOC], op=ALU.mult)
        nc.vector.tensor_reduce(out=rs[:], in_=rtmp[:], axis=AX.X, op=ALU.add)
        pu0 = weight_transposes(w_u[:, 0, :].bitcast(F32), "U0")
        pu1 = weight_transposes(w_u[:, 1, :].bitcast(F32), "U1")
        weight_copy("u", 0, pu0, False)
        quant_x(0, 0)
        weight_copy("u", 1, pu1, True)
        keep_tensor_busy()
        pw0 = weight_transposes(w_v[:, 0, :].bitcast(F32), "A")
        pw1 = weight_transposes(w_v[:, 1, :].bitcast(F32), "B")
        regroup_scalar(0, 1)
        weight_quant("u")
        regroup_vector(0, 1)
        weight_copy("v", 1, pw1, True)
        u_open(0)
        u_win(0, 0, 0, (0,))
        u_win(0, 1, 0, (0,))
        weight_copy("v", 0, pw0, False)
        quant_x(0, 1)
        pbv = psum.tile([P, CV], F32, tag="C1", name="pbv")
        nc.tensor.matmul(out=pbv[:], lhsT=ones[:], rhs=bvrow[:], start=True, stop=True)
        pw2 = weight_transposes(w_v[:, 2, :].bitcast(F32), "C0")
        pw3 = weight_transposes(w_v[:, 3, :].bitcast(F32), "U2")
        weight_copy("v", 2, pw2, False)
        weight_copy("v", 3, pw3, True)
        for k in range(2):
            nc.tensor.transpose(out=aux[:, 3 + k, :], in_=prm[:, k:256:2], identity=ident_b[:])
        u_open_tail(0)
        u_win(0, 0, 0, (1,))
        u_win(0, 1, 0, (1,))
        u_win(0, 0, 1)
        u_win(0, 0, 2)
        u_win(0, 1, 1)
        u_win(0, 1, 2)
        nc.scalar.copy(out=prmt[:].rearrange("p v k -> p k v"), in_=aux[:, 3:5, 0:5])
        nc.scalar.activation(out=sc[:], in_=prmt[:, 4, :], func=ACT.Sqrt, bias=eps[:, 0:1])
        weight_quant("v", 0, 1)
        nc.vector.tensor_sub(out=bi[:], in0=prmt[:, 0, :], in1=prmt[:, 3, :])
        nc.vector.reciprocal(out=sc[:], in_=sc[:])
        weight_quant("v", 1, 2)
        nc.vector.tensor_mul(out=sc[:], in0=sc[:], in1=prmt[:, 1, :])
        nc.scalar.copy(out=bvb[:], in_=pbv[:])
        px_mx(0, "X")
        px_mx(0, "Y")
        px_mx(0, "Z")
        cm_mx(0, 0)
        cm_mx(0, 1)
        regroup_vector(1, 0, (1,))
        nc.vector.tensor_mul(out=bi[:], in0=bi[:], in1=sc[:])
        regroup_vector(1, 0, (2, 3))
        nc.vector.tensor_add(out=bi[:], in0=bi[:], in1=prmt[:, 2, :])
        regroup_scalar(1, 0, (0,))
        px_copy(0, "X")
        regroup_scalar(1, 1, (0,))
        px_copy(0, "Y")
        px_copy(0, "Z")
        regroup_scalar(1, 1, (3,))
        regroup_vector(1, 1, (1, 2))
        quant_x(1, 0)
        cm_pool(0, 0)
        u_relu(0, 0)
        u_relu(0, 1)
        px_pool(0, "X")
        px_pool(0, "Y")
        px_pool(0, "Z")
        px_mx(1, "X", (0,))
        quant_x(1, 1)
        cm_pool(0, 1)
        cm_rows(0)
        u_open(1)
        u_open_tail(1)
        u_mx(1, 0)
        u_relu(1, 0)
        px_mx(1, "X", (1,))
        px_copy(1, "X")
        u_mx(1, 1)
        u_relu(1, 1)
        px_mx(1, "Y")
        px_copy(1, "Y")
        px_mx(1, "Z")
        px_copy(1, "Z")
        u_pool6(0, 0)
        u_pool6(0, 1)
        u_pool8(0, 0, 2)
        finish_px(0, 0)
        u_pool31(0)
        scale_keys(0, slice(0, 4))
        store_keys(0)
        u_pool6(1, 0)
        u_pool8(1, 0, 1)
        cm_total(0)
        px_pool(1, "X")
        px_pool(1, "Y")
        u_pool6(1, 1)
        u_pool8(1, 1, 2)
        scale_keys(1, slice(0, 1))
        u_pool31(1)
        scale_keys(1, slice(1, 4))
        store_keys(1)
        cm_transposes(0)
        px_pool(1, "Z")
        finish_cm(0)
        finish_px(1, 0)
        finish_px(1, 1)
